import numpy as np
import ml_dtypes


def mxq(x, axis, fmt="e4m3"):
    dtype, down = {"e4m3": (ml_dtypes.float8_e4m3fn, 7), "e5m2": (ml_dtypes.float8_e5m2, 14)}[fmt]
    v = np.moveaxis(np.asarray(x, np.float32).astype(ml_dtypes.bfloat16).astype(np.float64), axis, -1)
    blocks = v.reshape(v.shape[:-1] + (-1, 32))
    amax = np.abs(blocks).max(-1, keepdims=True)
    byte = np.maximum(np.where(amax > 0, np.frexp(amax)[1] - 1 + 127, 0) - down, 1)
    scale = np.exp2(byte - 127.0)
    codes = (blocks / scale).astype(np.float32).astype(dtype).astype(np.float64)
    return np.moveaxis((codes * scale).reshape(v.shape), -1, axis)


WIDE = False


def mx_kscale(k):
    if not WIDE:
        return np.ones(k)
    levels = np.array([10, -10, 5, -5, 0])
    a = np.random.permutation(np.resize(levels, k // 512 * 4)).reshape(k // 512, 4)
    idx = np.arange(k)
    return np.exp2(a[idx // 512, idx % 128 // 32])


BF16 = ml_dtypes.bfloat16


def bf(x):
    return np.asarray(x, np.float32).astype(BF16)


def f64(x):
    return np.asarray(x).astype(np.float64)


E2M1 = np.array([0.0, 0.5, 1.0, 1.5, 2.0, 3.0, 4.0, 6.0, -0.0, -0.5, -1.0, -1.5, -2.0, -3.0, -4.0, -6.0])


def pack_weight(w, fmt):
    k, n = w.shape
    w = f64(bf(w)).reshape(k // 32, 32, n)
    amax = np.abs(w).max(1)
    if fmt == "e4m3":
        byte = np.frexp(amax)[1] - 1 + 127 - 7
    else:
        mant, ex = np.frexp(amax / 6.0)
        byte = np.where(mant > 0.5, ex, ex - 1) + 127
    byte = np.clip(np.where(amax > 0, byte, 1), 1, 254)
    scaled = (w * np.exp2(127.0 - byte)[:, None, :]).reshape(k, n).astype(np.float32)
    by_word = np.ascontiguousarray(scaled.reshape(k // 512, 128, 4, n).transpose(0, 1, 3, 2))
    if fmt == "e4m3":
        words = by_word.astype(ml_dtypes.float8_e4m3fn).view(np.uint8)
    else:
        c = by_word.astype(ml_dtypes.float4_e2m1fn).view(np.uint8) & 0xF
        words = c[..., 0::2] | (c[..., 1::2] << 4)
    return np.ascontiguousarray(words), np.ascontiguousarray(byte.astype(np.uint8).reshape(k // 512, 16, n))


def unpack_weight(words, scales, fmt):
    g, p, n, _ = words.shape
    if fmt == "e4m3":
        vals = np.ascontiguousarray(words).view(ml_dtypes.float8_e4m3fn).astype(np.float64)
    else:
        nib = np.empty((g, p, n, 4), np.uint8)
        nib[..., 0::2] = words & 0xF
        nib[..., 1::2] = words >> 4
        vals = E2M1[nib]
    vals = vals * np.repeat(np.exp2(scales.astype(np.float64) - 127.0), 8, axis=1)[..., None]
    return vals.transpose(0, 1, 3, 2).reshape(g * 512, n)


B, S, D, E, F, NH, BAND = 4, 256, 512, 512, 1024, 4, 6
HL = D // NH
HG = E // NH
EPS = 1e-5
FMT = "e4m3"


def layernorm(x, w, b):
    m = x.mean(-1, keepdims=True)
    v = ((x - m) ** 2).mean(-1, keepdims=True)
    return (x - m) / np.sqrt(v + EPS) * w + b


def heads(t):
    return t.reshape(B, S, NH, HG).transpose(0, 2, 1, 3)


def setup_inputs():
    r = np.random.standard_normal
    s = mx_kscale(D)
    o_loc = bf(r((B, NH, S, HL)) * 0.5 * s.reshape(NH, 1, HL))
    x = bf(r((B, S, D)))
    Wo_l = r((D, D)) / np.sqrt(D) / s
    bo_l = bf(r(D) * 0.1)
    ln2_w = bf(1.0 + 0.1 * r(D))
    ln2_b = bf(r(D) * 0.1)
    Wqkv_g = r((3 * E, D)) * 1.4 / np.sqrt(D)
    bqkv_g = bf(r(3 * E) * 0.1)
    Wo_l_words, Wo_l_scales = pack_weight(np.ascontiguousarray(Wo_l.T), FMT)
    Wqkv_g_words, Wqkv_g_scales = pack_weight(np.ascontiguousarray(Wqkv_g.T), FMT)
    return {
        "o_loc": o_loc,
        "x": x,
        "Wo_l_words": Wo_l_words,
        "Wo_l_scales": Wo_l_scales,
        "bo_l": bo_l,
        "ln2_w": ln2_w,
        "ln2_b": ln2_b,
        "Wqkv_g_words": Wqkv_g_words,
        "Wqkv_g_scales": Wqkv_g_scales,
        "bqkv_g": bqkv_g,
    }


def reference(o_loc, x, Wo_l_words, Wo_l_scales, bo_l, ln2_w, ln2_b, Wqkv_g_words, Wqkv_g_scales, bqkv_g):
    o = f64(o_loc).transpose(0, 2, 1, 3).reshape(B, S, D)
    x_loc = f64(x) + ((mxq(o, 2, "e4m3") @ unpack_weight(Wo_l_words, Wo_l_scales, FMT)) + f64(bo_l))
    h = layernorm(x_loc, f64(ln2_w), f64(ln2_b))
    qkv = (mxq(h, 2, "e4m3") @ unpack_weight(Wqkv_g_words, Wqkv_g_scales, FMT)) + f64(bqkv_g)
    q, k, v = np.split(qkv, 3, axis=-1)
    return x_loc, heads(q), heads(k), heads(v)

@@ -1,0 +1,296 @@
+from contextlib import ExitStack
+
+import concourse.masks as masks
+import concourse.mybir as mybir
+
+F32 = mybir.dt.float32
+BF16 = mybir.dt.bfloat16
+I32 = mybir.dt.int32
+U32 = mybir.dt.uint32
+U8 = mybir.dt.uint8
+FP8X4 = mybir.dt.float8_e4m3fn_x4
+ALU = mybir.AluOpType
+ACT = mybir.ActivationFunctionType
+
+B, S, D, NH, HD = 4, 256, 512, 4, 128
+P = 128
+R = S // P
+PACK = 4
+PAIR = 2
+N_QKV = 3
+N_ALL = D + N_QKV * D
+BLOCK_ROWS = 16
+EPS = 1e-5
+RESID_ON_VECTOR = 1
+FLOPS = 2 * B * S * D * N_ALL
+
+
+def tile_block_pa_kernel(
+    tc,
+    o_loc,
+    x,
+    Wo_l_words,
+    Wo_l_scales,
+    bo_l,
+    ln2_w,
+    ln2_b,
+    Wqkv_g_words,
+    Wqkv_g_scales,
+    bqkv_g,
+    out_0,
+    out_1,
+    out_2,
+    out_3,
+):
+    nc = tc.nc
+    qkv_out = [out_1, out_2, out_3]
+
+    with ExitStack() as ctx:
+        const = ctx.enter_context(tc.tile_pool(name="const", bufs=1))
+        batch = ctx.enter_context(tc.tile_pool(name="batch", bufs=B))
+        work = ctx.enter_context(tc.tile_pool(name="work", bufs=2))
+        heads = ctx.enter_context(tc.tile_pool(name="heads", bufs=2 * N_QKV))
+        psum_o = ctx.enter_context(tc.psum_pool(name="psum_o", bufs=1))
+        psum_x = ctx.enter_context(tc.psum_pool(name="psum_x", bufs=2))
+        psum_h = ctx.enter_context(tc.psum_pool(name="psum_h", bufs=2))
+        psum_qkv = ctx.enter_context(tc.psum_pool(name="psum_qkv", bufs=3))
+
+        o_sb = {}
+        x_sb = {}
+
+        def load_batch(b):
+            o_b = batch.tile([P, R, D], BF16)
+            by_r = o_loc[b].rearrange("n (p r) d -> r p n d", r=R)
+            for r in range(R):
+                nc.sync.dma_start(out=o_b[:, r, :].rearrange("p (n d) -> p n d", n=NH), in_=by_r[r])
+            x_b = batch.tile([P, R, D], BF16)
+            nc.sync.dma_start(
+                out=x_b[:].rearrange("p r k -> p (r k)"),
+                in_=x[b].rearrange("(p r) k -> p (r k)", r=R),
+            )
+            o_sb[b] = o_b
+            x_sb[b] = x_b
+
+        w_scales = const.tile([P, N_ALL], U8, align_bytes=64)
+        nc.vector.memset(w_scales[:].bitcast(I32), 0)
+
+        def load_scales(rows, cols):
+            for j in range(4):
+                nc.sync.dma_start(
+                    out=w_scales[j:P:32, cols].bitcast(I32),
+                    in_=rows[j:BLOCK_ROWS:4, :].bitcast(I32),
+                )
+
+        wo_words = const.tile([P, D], U32, align_bytes=64)
+        wqkv_words = const.tile([P, N_QKV * D], U32, align_bytes=64)
+
+        bo_rows = const.tile([P, D], BF16)
+        nc.vector.memset(bo_rows[:], 0.0)
+        ones = const.tile([P, P], BF16)
+        nc.vector.memset(ones[:], 1.0)
+        bqkv_rows = const.tile([P, N_QKV * D], BF16)
+        nc.vector.memset(bqkv_rows[:], 0.0)
+        gain_bf = const.tile([P, PACK], BF16)
+        shift_bf = const.tile([P, PACK], BF16)
+
+        load_scales(Wo_l_scales[0], slice(0, D))
+        nc.sync.dma_start(out=bo_rows[0:1, :], in_=bo_l.rearrange("(o n) -> o n", o=1))
+        load_batch(0)
+        nc.sync.dma_start(
+            out=wo_words[:].bitcast(I32),
+            in_=Wo_l_words[0].rearrange("p n t -> p (n t)").bitcast(I32),
+        )
+        nc.sync.dma_start(out=gain_bf[:], in_=ln2_w.rearrange("(p t) -> p t", t=PACK))
+        nc.sync.dma_start(out=shift_bf[:], in_=ln2_b.rearrange("(p t) -> p t", t=PACK))
+        load_batch(1)
+        nc.sync.dma_start(out=bqkv_rows[0:1, :], in_=bqkv_g.rearrange("(o n) -> o n", o=1))
+        load_scales(Wqkv_g_scales[0], slice(D, N_ALL))
+        nc.sync.dma_start(
+            out=wqkv_words[:].bitcast(I32),
+            in_=Wqkv_g_words[0].rearrange("p n t -> p (n t)").bitcast(I32),
+        )
+        load_batch(2)
+        load_batch(3)
+
+        bias_all = const.tile([P, N_ALL], F32)
+
+        def spread_bias(rows, first_col):
+            for j in range(rows.shape[1] // D):
+                spread = psum_qkv.tile([P, D], F32, tag="qkv_acc")
+                nc.tensor.matmul(
+                    out=spread[:], lhsT=ones[:], rhs=rows[:, j * D : (j + 1) * D], start=True, stop=True
+                )
+                nc.scalar.copy(out=bias_all[:, first_col + j * D : first_col + (j + 1) * D], in_=spread[:])
+
+        gain = const.tile([P, PACK], F32)
+        shift = const.tile([P, PACK], F32)
+        nc.gpsimd.tensor_copy(out=gain[:], in_=gain_bf[:])
+        nc.gpsimd.tensor_copy(out=shift[:], in_=shift_bf[:])
+
+        identity = const.tile([P, P], F32)
+        masks.make_identity(nc, identity[:])
+        minus_half = const.tile([P, R], F32)
+        nc.vector.memset(minus_half[:], -0.5)
+
+        x_loc = {}
+        minus_mean = {}
+        normed = {}
+        h_codes = {}
+        h_scales = {}
+
+        def project_heads(b):
+            adder = nc.vector if b < RESID_ON_VECTOR else nc.gpsimd
+            resid = batch.tile([P, R, D], F32)
+            for r in range(R):
+                adder.tensor_tensor(
+                    out=resid[:, r, :], in0=x_sb[b][:, r, :], in1=bias_all[:, 0:D], op=ALU.add
+                )
+
+            o_t = psum_o.tile([P, R, PAIR, P], F32)
+            for r in range(R):
+                words = o_sb[b][:, r, :].bitcast(F32)
+                for u in range(PAIR):
+                    nc.tensor.transpose(
+                        out=o_t[:, r, u, :], in_=words[:, u : D // PAIR : PAIR], identity=identity[:]
+                    )
+            o_grouped = work.tile([P, R * P * PACK], BF16, align_bytes=64)
+            nc.scalar.copy(
+                out=o_grouped[:].bitcast(F32).rearrange("p (r c u) -> p r c u", r=R, u=PAIR),
+                in_=o_t[:].rearrange("p r u c -> p r c u"),
+            )
+            o_codes = work.tile([P, R * P], U32, align_bytes=64)
+            o_scales = work.tile([P, R * P], U8, align_bytes=64)
+            nc.vector.quantize_mx(out=o_codes[:].bitcast(FP8X4), scales=o_scales[:], in_=o_grouped[:])
+
+            x_loc_b = batch.tile([P, R, D], F32)
+            token_sum = batch.tile([P, R], F32)
+            minus_mean_b = batch.tile([P, R], F32)
+            for r in range(R):
+                tokens = slice(r * P, (r + 1) * P)
+                x_acc = psum_x.tile([P, D], F32)
+                nc.tensor.matmul_mx(
+                    out=x_acc[:],
+                    lhsT=o_codes[:, tokens].bitcast(FP8X4),
+                    lhsT_scale=o_scales[:, tokens],
+                    rhs=wo_words[:].bitcast(FP8X4),
+                    rhs_scale=w_scales[:, 0:D],
+                    start=True,
+                    stop=True,
+                )
+                nc.vector.scalar_tensor_tensor(
+                    out=x_loc_b[:, r, :],
+                    in0=x_acc[:],
+                    scalar=1.0,
+                    in1=resid[:, r, :],
+                    op0=ALU.mult,
+                    op1=ALU.add,
+                    accum_out=token_sum[:, r : r + 1],
+                )
+                nc.scalar.mul(
+                    out=minus_mean_b[:, r : r + 1], in_=token_sum[:, r : r + 1], mul=-1.0 / D
+                )
+            nc.sync.dma_start(
+                out=out_0[b].rearrange("(p r) k -> p (r k)", r=R),
+                in_=x_loc_b[:].rearrange("p r k -> p (r k)"),
+            )
+            x_loc[b] = x_loc_b
+            minus_mean[b] = minus_mean_b
+
+        def normalise(b):
+            squares = work.tile([P, R, D], BF16)
+            sum_sq = batch.tile([P, R], F32)
+            var_eps = batch.tile([P, R], F32)
+            rstd = batch.tile([P, R], F32)
+            normed_b = work.tile([P, R, PACK, P], F32)
+            for r in range(R):
+                one = slice(r, r + 1)
+                nc.scalar.activation(
+                    out=squares[:, r, :],
+                    in_=x_loc[b][:, r, :],
+                    func=ACT.Square,
+                    bias=minus_mean[b][:, one],
+                    scale=1.0,
+                    accum_out=sum_sq[:, one],
+                )
+                nc.gpsimd.tensor_scalar(
+                    out=var_eps[:, one], in0=sum_sq[:, one], scalar1=1.0 / D, scalar2=EPS, op0=ALU.mult, op1=ALU.add
+                )
+                nc.gpsimd.tensor_tensor(out=rstd[:, one], in0=var_eps[:, one], in1=minus_half[:, one], op=ALU.pow)
+                nc.gpsimd.tensor_scalar(
+                    out=normed_b[:, r, :, :],
+                    in0=x_loc[b][:, r, :].rearrange("p (q t) -> p t q", t=PACK),
+                    scalar1=minus_mean[b][:, one],
+                    scalar2=rstd[:, one],
+                    op0=ALU.add,
+                    op1=ALU.mult,
+                )
+            normed[b] = normed_b
+
+        def quantise_h(b):
+            h_t = work.tile([P, PACK, R * P], BF16)
+            for half in range(PACK // 2):
+                normed_t = psum_h.tile([P, 2, R, P], F32)
+                for i in range(2):
+                    for r in range(R):
+                        nc.tensor.transpose(
+                            out=normed_t[:, i, r, :],
+                            in_=normed[b][:, r, 2 * half + i, :],
+                            identity=identity[:],
+                        )
+                for i in range(2):
+                    t = 2 * half + i
+                    nc.scalar.activation(
+                        out=h_t[:, t, :],
+                        in_=normed_t[:, i, :, :].rearrange("p r c -> p (r c)"),
+                        func=ACT.Identity,
+                        scale=gain[:, t : t + 1],
+                        bias=shift[:, t : t + 1],
+                    )
+            h_grouped = work.tile([P, R * P, PACK], BF16, align_bytes=64)
+            nc.vector.tensor_copy(out=h_grouped[:], in_=h_t[:].rearrange("p t c -> p c t"))
+            h_codes_b = work.tile([P, R * P], U32, align_bytes=64)
+            h_scales_b = work.tile([P, R * P], U8, align_bytes=64)
+            nc.vector.quantize_mx(
+                out=h_codes_b[:].bitcast(FP8X4),
+                scales=h_scales_b[:],
+                in_=h_grouped[:].rearrange("p c t -> p (c t)"),
+            )
+            h_codes[b] = h_codes_b
+            h_scales[b] = h_scales_b
+
+        def project_qkv(b):
+            for w in range(N_QKV):
+                cols = slice(D + w * D, D + (w + 1) * D)
+                head_rows = heads.tile([P, NH, R, HD], F32)
+                for r in range(R):
+                    tokens = slice(r * P, (r + 1) * P)
+                    qkv_acc = psum_qkv.tile([P, D], F32, tag="qkv_acc")
+                    nc.tensor.matmul_mx(
+                        out=qkv_acc[:],
+                        lhsT=h_codes[b][:, tokens].bitcast(FP8X4),
+                        lhsT_scale=h_scales[b][:, tokens],
+                        rhs=wqkv_words[:, w * D : (w + 1) * D].bitcast(FP8X4),
+                        rhs_scale=w_scales[:, cols],
+                        start=True,
+                        stop=True,
+                    )
+                    nc.vector.tensor_tensor(
+                        out=head_rows[:, :, r, :],
+                        in0=qkv_acc[:].rearrange("p (n d) -> p n d", n=NH),
+                        in1=bias_all[:, cols].rearrange("p (n d) -> p n d", n=NH),
+                        op=ALU.add,
+                    )
+                nc.sync.dma_start(
+                    out=qkv_out[w][b].rearrange("n (p r) d -> p n (r d)", r=R),
+                    in_=head_rows[:].rearrange("p n r d -> p n (r d)"),
+                )
+
+        spread_bias(bo_rows, 0)
+        stages = [project_heads, normalise, quantise_h, project_qkv]
+        for step in range(B + len(stages) - 1):
+            for i, stage in enumerate(stages):
+                b = step - i
+                if 0 <= b < B:
+                    stage(b)
+            if step == 0:
+                spread_bias(bqkv_rows, D)

@@ -15,13 +15,14 @@ ACT = mybir.ActivationFunctionType
 B, S, D, NH, HD = 4, 256, 512, 4, 128
 P = 128
 R = S // P
+TILES = B * R
 PACK = 4
 PAIR = 2
 N_QKV = 3
 N_ALL = D + N_QKV * D
 BLOCK_ROWS = 16
 EPS = 1e-5
-RESID_ON_VECTOR = 1
+RESID_ON_VECTOR = 8
 FLOPS = 2 * B * S * D * N_ALL
 
 
@@ -48,7 +49,7 @@ def tile_block_pa_kernel(
     with ExitStack() as ctx:
         const = ctx.enter_context(tc.tile_pool(name="const", bufs=1))
         batch = ctx.enter_context(tc.tile_pool(name="batch", bufs=B))
-        work = ctx.enter_context(tc.tile_pool(name="work", bufs=2))
+        group = ctx.enter_context(tc.tile_pool(name="group", bufs=8))
         heads = ctx.enter_context(tc.tile_pool(name="heads", bufs=2 * N_QKV))
         psum_o = ctx.enter_context(tc.psum_pool(name="psum_o", bufs=1))
         psum_x = ctx.enter_context(tc.psum_pool(name="psum_x", bufs=2))
@@ -84,6 +85,11 @@ def tile_block_pa_kernel(
         wo_words = const.tile([P, D], U32, align_bytes=64)
         wqkv_words = const.tile([P, N_QKV * D], U32, align_bytes=64)
 
+        def load_words(words, packed):
+            nc.sync.dma_start(
+                out=words[:].bitcast(I32), in_=packed[0].rearrange("p n t -> p (n t)").bitcast(I32)
+            )
+
         bo_rows = const.tile([P, D], BF16)
         nc.vector.memset(bo_rows[:], 0.0)
         ones = const.tile([P, P], BF16)
@@ -95,20 +101,14 @@ def tile_block_pa_kernel(
 
         load_scales(Wo_l_scales[0], slice(0, D))
         nc.sync.dma_start(out=bo_rows[0:1, :], in_=bo_l.rearrange("(o n) -> o n", o=1))
+        load_words(wo_words, Wo_l_words)
         load_batch(0)
-        nc.sync.dma_start(
-            out=wo_words[:].bitcast(I32),
-            in_=Wo_l_words[0].rearrange("p n t -> p (n t)").bitcast(I32),
-        )
         nc.sync.dma_start(out=gain_bf[:], in_=ln2_w.rearrange("(p t) -> p t", t=PACK))
         nc.sync.dma_start(out=shift_bf[:], in_=ln2_b.rearrange("(p t) -> p t", t=PACK))
         load_batch(1)
         nc.sync.dma_start(out=bqkv_rows[0:1, :], in_=bqkv_g.rearrange("(o n) -> o n", o=1))
         load_scales(Wqkv_g_scales[0], slice(D, N_ALL))
-        nc.sync.dma_start(
-            out=wqkv_words[:].bitcast(I32),
-            in_=Wqkv_g_words[0].rearrange("p n t -> p (n t)").bitcast(I32),
-        )
+        load_words(wqkv_words, Wqkv_g_words)
         load_batch(2)
         load_batch(3)
 
@@ -122,14 +122,13 @@ def tile_block_pa_kernel(
                 )
                 nc.scalar.copy(out=bias_all[:, first_col + j * D : first_col + (j + 1) * D], in_=spread[:])
 
+        identity = const.tile([P, P], F32)
+        masks.make_identity(nc, identity[:])
         gain = const.tile([P, PACK], F32)
         shift = const.tile([P, PACK], F32)
         nc.gpsimd.tensor_copy(out=gain[:], in_=gain_bf[:])
         nc.gpsimd.tensor_copy(out=shift[:], in_=shift_bf[:])
-
-        identity = const.tile([P, P], F32)
-        masks.make_identity(nc, identity[:])
-        minus_half = const.tile([P, R], F32)
+        minus_half = const.tile([P, 1], F32)
         nc.vector.memset(minus_half[:], -0.5)
 
         x_loc = {}
@@ -138,137 +137,124 @@ def tile_block_pa_kernel(
         h_codes = {}
         h_scales = {}
 
-        def project_heads(b):
-            adder = nc.vector if b < RESID_ON_VECTOR else nc.gpsimd
-            resid = batch.tile([P, R, D], F32)
-            for r in range(R):
-                adder.tensor_tensor(
-                    out=resid[:, r, :], in0=x_sb[b][:, r, :], in1=bias_all[:, 0:D], op=ALU.add
-                )
+        def project_heads(j):
+            b, r = divmod(j, R)
+            adder = nc.vector if j < RESID_ON_VECTOR else nc.gpsimd
+            resid = group.tile([P, D], F32)
+            adder.tensor_tensor(out=resid[:], in0=x_sb[b][:, r, :], in1=bias_all[:, 0:D], op=ALU.add)
 
-            o_t = psum_o.tile([P, R, PAIR, P], F32)
-            for r in range(R):
-                words = o_sb[b][:, r, :].bitcast(F32)
-                for u in range(PAIR):
-                    nc.tensor.transpose(
-                        out=o_t[:, r, u, :], in_=words[:, u : D // PAIR : PAIR], identity=identity[:]
-                    )
-            o_grouped = work.tile([P, R * P * PACK], BF16, align_bytes=64)
+            o_t = psum_o.tile([P, PAIR, P], F32)
+            words = o_sb[b][:, r, :].bitcast(F32)
+            for u in range(PAIR):
+                nc.tensor.transpose(
+                    out=o_t[:, u, :], in_=words[:, u : D // PAIR : PAIR], identity=identity[:]
+                )
+            o_grouped = group.tile([P, P * PACK], BF16, align_bytes=64)
             nc.scalar.copy(
-                out=o_grouped[:].bitcast(F32).rearrange("p (r c u) -> p r c u", r=R, u=PAIR),
-                in_=o_t[:].rearrange("p r u c -> p r c u"),
+                out=o_grouped[:].bitcast(F32).rearrange("p (c u) -> p c u", u=PAIR),
+                in_=o_t[:].rearrange("p u c -> p c u"),
             )
-            o_codes = work.tile([P, R * P], U32, align_bytes=64)
-            o_scales = work.tile([P, R * P], U8, align_bytes=64)
+            o_codes = group.tile([P, P], U32, align_bytes=64)
+            o_scales = group.tile([P, P], U8, align_bytes=64)
             nc.vector.quantize_mx(out=o_codes[:].bitcast(FP8X4), scales=o_scales[:], in_=o_grouped[:])
 
-            x_loc_b = batch.tile([P, R, D], F32)
-            token_sum = batch.tile([P, R], F32)
-            minus_mean_b = batch.tile([P, R], F32)
-            for r in range(R):
-                tokens = slice(r * P, (r + 1) * P)
-                x_acc = psum_x.tile([P, D], F32)
-                nc.tensor.matmul_mx(
-                    out=x_acc[:],
-                    lhsT=o_codes[:, tokens].bitcast(FP8X4),
-                    lhsT_scale=o_scales[:, tokens],
-                    rhs=wo_words[:].bitcast(FP8X4),
-                    rhs_scale=w_scales[:, 0:D],
-                    start=True,
-                    stop=True,
-                )
-                nc.vector.scalar_tensor_tensor(
-                    out=x_loc_b[:, r, :],
-                    in0=x_acc[:],
-                    scalar=1.0,
-                    in1=resid[:, r, :],
-                    op0=ALU.mult,
-                    op1=ALU.add,
-                    accum_out=token_sum[:, r : r + 1],
-                )
-                nc.scalar.mul(
-                    out=minus_mean_b[:, r : r + 1], in_=token_sum[:, r : r + 1], mul=-1.0 / D
-                )
-            nc.sync.dma_start(
-                out=out_0[b].rearrange("(p r) k -> p (r k)", r=R),
-                in_=x_loc_b[:].rearrange("p r k -> p (r k)"),
+            x_acc = psum_x.tile([P, D], F32)
+            nc.tensor.matmul_mx(
+                out=x_acc[:],
+                lhsT=o_codes[:].bitcast(FP8X4),
+                lhsT_scale=o_scales[:],
+                rhs=wo_words[:].bitcast(FP8X4),
+                rhs_scale=w_scales[:, 0:D],
+                start=True,
+                stop=True,
             )
-            x_loc[b] = x_loc_b
-            minus_mean[b] = minus_mean_b
+            if r == 0:
+                x_loc_b = batch.tile([P, R, D], F32)
+                x_loc[b] = x_loc_b
+            token_sum = group.tile([P, 1], F32)
+            nc.vector.scalar_tensor_tensor(
+                out=x_loc[b][:, r, :],
+                in0=x_acc[:],
+                scalar=1.0,
+                in1=resid[:],
+                op0=ALU.mult,
+                op1=ALU.add,
+                accum_out=token_sum[:],
+            )
+            if r == R - 1:
+                nc.sync.dma_start(
+                    out=out_0[b].rearrange("(p r) k -> p (r k)", r=R),
+                    in_=x_loc[b][:].rearrange("p r k -> p (r k)"),
+                )
+            minus_mean_j = group.tile([P, 1], F32)
+            nc.scalar.mul(out=minus_mean_j[:], in_=token_sum[:], mul=-1.0 / D)
+            minus_mean[j] = minus_mean_j
 
-        def normalise(b):
-            squares = work.tile([P, R, D], BF16)
-            sum_sq = batch.tile([P, R], F32)
-            var_eps = batch.tile([P, R], F32)
-            rstd = batch.tile([P, R], F32)
-            normed_b = work.tile([P, R, PACK, P], F32)
-            for r in range(R):
-                one = slice(r, r + 1)
+        def normalise(j):
+            b, r = divmod(j, R)
+            squares = group.tile([P, D], BF16)
+            sum_sq = group.tile([P, 1], F32)
+            nc.scalar.activation(
+                out=squares[:],
+                in_=x_loc[b][:, r, :],
+                func=ACT.Square,
+                bias=minus_mean[j][:],
+                scale=1.0,
+                accum_out=sum_sq[:],
+            )
+            var_eps = group.tile([P, 1], F32)
+            nc.gpsimd.tensor_scalar(
+                out=var_eps[:], in0=sum_sq[:], scalar1=1.0 / D, scalar2=EPS, op0=ALU.mult, op1=ALU.add
+            )
+            rstd = group.tile([P, 1], F32)
+            nc.gpsimd.tensor_tensor(out=rstd[:], in0=var_eps[:], in1=minus_half[:], op=ALU.pow)
+            normed_j = group.tile([P, PACK, P], F32)
+            nc.gpsimd.tensor_scalar(
+                out=normed_j[:],
+                in0=x_loc[b][:, r, :].rearrange("p (q t) -> p t q", t=PACK),
+                scalar1=minus_mean[j][:],
+                scalar2=rstd[:],
+                op0=ALU.add,
+                op1=ALU.mult,
+            )
+            normed[j] = normed_j
+
+        def quantise_h(j):
+            normed_t = psum_h.tile([P, PACK, P], F32)
+            for t in range(PACK):
+                nc.tensor.transpose(out=normed_t[:, t, :], in_=normed[j][:, t, :], identity=identity[:])
+            h_t = group.tile([P, PACK, P], BF16)
+            for t in range(PACK):
                 nc.scalar.activation(
-                    out=squares[:, r, :],
-                    in_=x_loc[b][:, r, :],
-                    func=ACT.Square,
-                    bias=minus_mean[b][:, one],
-                    scale=1.0,
-                    accum_out=sum_sq[:, one],
+                    out=h_t[:, t, :],
+                    in_=normed_t[:, t, :],
+                    func=ACT.Identity,
+                    scale=gain[:, t : t + 1],
+                    bias=shift[:, t : t + 1],
                 )
-                nc.gpsimd.tensor_scalar(
-                    out=var_eps[:, one], in0=sum_sq[:, one], scalar1=1.0 / D, scalar2=EPS, op0=ALU.mult, op1=ALU.add
-                )
-                nc.gpsimd.tensor_tensor(out=rstd[:, one], in0=var_eps[:, one], in1=minus_half[:, one], op=ALU.pow)
-                nc.gpsimd.tensor_scalar(
-                    out=normed_b[:, r, :, :],
-                    in0=x_loc[b][:, r, :].rearrange("p (q t) -> p t q", t=PACK),
-                    scalar1=minus_mean[b][:, one],
-                    scalar2=rstd[:, one],
-                    op0=ALU.add,
-                    op1=ALU.mult,
-                )
-            normed[b] = normed_b
-
-        def quantise_h(b):
-            h_t = work.tile([P, PACK, R * P], BF16)
-            for half in range(PACK // 2):
-                normed_t = psum_h.tile([P, 2, R, P], F32)
-                for i in range(2):
-                    for r in range(R):
-                        nc.tensor.transpose(
-                            out=normed_t[:, i, r, :],
-                            in_=normed[b][:, r, 2 * half + i, :],
-                            identity=identity[:],
-                        )
-                for i in range(2):
-                    t = 2 * half + i
-                    nc.scalar.activation(
-                        out=h_t[:, t, :],
-                        in_=normed_t[:, i, :, :].rearrange("p r c -> p (r c)"),
-                        func=ACT.Identity,
-                        scale=gain[:, t : t + 1],
-                        bias=shift[:, t : t + 1],
-                    )
-            h_grouped = work.tile([P, R * P, PACK], BF16, align_bytes=64)
-            nc.vector.tensor_copy(out=h_grouped[:], in_=h_t[:].rearrange("p t c -> p c t"))
-            h_codes_b = work.tile([P, R * P], U32, align_bytes=64)
-            h_scales_b = work.tile([P, R * P], U8, align_bytes=64)
+            h_grouped = group.tile([P, P, PACK], BF16, align_bytes=64)
+            nc.scalar.copy(out=h_grouped[:], in_=h_t[:].rearrange("p t c -> p c t"))
+            h_codes_j = group.tile([P, P], U32, align_bytes=64)
+            h_scales_j = group.tile([P, P], U8, align_bytes=64)
             nc.vector.quantize_mx(
-                out=h_codes_b[:].bitcast(FP8X4),
-                scales=h_scales_b[:],
+                out=h_codes_j[:].bitcast(FP8X4),
+                scales=h_scales_j[:],
                 in_=h_grouped[:].rearrange("p c t -> p (c t)"),
             )
-            h_codes[b] = h_codes_b
-            h_scales[b] = h_scales_b
+            h_codes[j] = h_codes_j
+            h_scales[j] = h_scales_j
 
         def project_qkv(b):
             for w in range(N_QKV):
                 cols = slice(D + w * D, D + (w + 1) * D)
                 head_rows = heads.tile([P, NH, R, HD], F32)
                 for r in range(R):
-                    tokens = slice(r * P, (r + 1) * P)
+                    j = R * b + r
                     qkv_acc = psum_qkv.tile([P, D], F32, tag="qkv_acc")
                     nc.tensor.matmul_mx(
                         out=qkv_acc[:],
-                        lhsT=h_codes[b][:, tokens].bitcast(FP8X4),
-                        lhsT_scale=h_scales[b][:, tokens],
+                        lhsT=h_codes[j][:].bitcast(FP8X4),
+                        lhsT_scale=h_scales[j][:],
                         rhs=wqkv_words[:, w * D : (w + 1) * D].bitcast(FP8X4),
                         rhs_scale=w_scales[:, cols],
                         start=True,
@@ -286,11 +272,14 @@ def tile_block_pa_kernel(
                 )
 
         spread_bias(bo_rows, 0)
-        stages = [project_heads, normalise, quantise_h, project_qkv]
-        for step in range(B + len(stages) - 1):
-            for i, stage in enumerate(stages):
-                b = step - i
-                if 0 <= b < B:
-                    stage(b)
-            if step == 0:
+        for step in range(TILES + 8):
+            if step < TILES:
+                project_heads(step)
+            if step == 1:
                 spread_bias(bqkv_rows, D)
+            if 0 <= step - 1 < TILES:
+                normalise(step - 1)
+            if 0 <= step - 2 < TILES:
+                quantise_h(step - 2)
+            if 0 <= step - 8 < TILES and (step - 8) % R == R - 1:
+                project_qkv((step - 8) // R)

@@ -15,14 +15,13 @@ ACT = mybir.ActivationFunctionType
 B, S, D, NH, HD = 4, 256, 512, 4, 128
 P = 128
 R = S // P
-TILES = B * R
 PACK = 4
 PAIR = 2
 N_QKV = 3
 N_ALL = D + N_QKV * D
 BLOCK_ROWS = 16
 EPS = 1e-5
-RESID_ON_VECTOR = 8
+RESID_ON_VECTOR = 4
 FLOPS = 2 * B * S * D * N_ALL
 
 
@@ -49,7 +48,7 @@ def tile_block_pa_kernel(
     with ExitStack() as ctx:
         const = ctx.enter_context(tc.tile_pool(name="const", bufs=1))
         batch = ctx.enter_context(tc.tile_pool(name="batch", bufs=B))
-        group = ctx.enter_context(tc.tile_pool(name="group", bufs=8))
+        work = ctx.enter_context(tc.tile_pool(name="work", bufs=2))
         heads = ctx.enter_context(tc.tile_pool(name="heads", bufs=2 * N_QKV))
         psum_o = ctx.enter_context(tc.psum_pool(name="psum_o", bufs=1))
         psum_x = ctx.enter_context(tc.psum_pool(name="psum_x", bufs=2))
@@ -85,11 +84,6 @@ def tile_block_pa_kernel(
         wo_words = const.tile([P, D], U32, align_bytes=64)
         wqkv_words = const.tile([P, N_QKV * D], U32, align_bytes=64)
 
-        def load_words(words, packed):
-            nc.sync.dma_start(
-                out=words[:].bitcast(I32), in_=packed[0].rearrange("p n t -> p (n t)").bitcast(I32)
-            )
-
         bo_rows = const.tile([P, D], BF16)
         nc.vector.memset(bo_rows[:], 0.0)
         ones = const.tile([P, P], BF16)
@@ -101,14 +95,20 @@ def tile_block_pa_kernel(
 
         load_scales(Wo_l_scales[0], slice(0, D))
         nc.sync.dma_start(out=bo_rows[0:1, :], in_=bo_l.rearrange("(o n) -> o n", o=1))
-        load_words(wo_words, Wo_l_words)
+        nc.sync.dma_start(
+            out=wo_words[:].bitcast(I32),
+            in_=Wo_l_words[0].rearrange("p n t -> p (n t)").bitcast(I32),
+        )
         load_batch(0)
         nc.sync.dma_start(out=gain_bf[:], in_=ln2_w.rearrange("(p t) -> p t", t=PACK))
         nc.sync.dma_start(out=shift_bf[:], in_=ln2_b.rearrange("(p t) -> p t", t=PACK))
         load_batch(1)
         nc.sync.dma_start(out=bqkv_rows[0:1, :], in_=bqkv_g.rearrange("(o n) -> o n", o=1))
         load_scales(Wqkv_g_scales[0], slice(D, N_ALL))
-        load_words(wqkv_words, Wqkv_g_words)
+        nc.sync.dma_start(
+            out=wqkv_words[:].bitcast(I32),
+            in_=Wqkv_g_words[0].rearrange("p n t -> p (n t)").bitcast(I32),
+        )
         load_batch(2)
         load_batch(3)
 
@@ -122,13 +122,14 @@ def tile_block_pa_kernel(
                 )
                 nc.scalar.copy(out=bias_all[:, first_col + j * D : first_col + (j + 1) * D], in_=spread[:])
 
-        identity = const.tile([P, P], F32)
-        masks.make_identity(nc, identity[:])
         gain = const.tile([P, PACK], F32)
         shift = const.tile([P, PACK], F32)
         nc.gpsimd.tensor_copy(out=gain[:], in_=gain_bf[:])
         nc.gpsimd.tensor_copy(out=shift[:], in_=shift_bf[:])
-        minus_half = const.tile([P, 1], F32)
+
+        identity = const.tile([P, P], F32)
+        masks.make_identity(nc, identity[:])
+        minus_half = const.tile([P, R], F32)
         nc.vector.memset(minus_half[:], -0.5)
 
         x_loc = {}
@@ -137,124 +138,137 @@ def tile_block_pa_kernel(
         h_codes = {}
         h_scales = {}
 
-        def project_heads(j):
-            b, r = divmod(j, R)
-            adder = nc.vector if j < RESID_ON_VECTOR else nc.gpsimd
-            resid = group.tile([P, D], F32)
-            adder.tensor_tensor(out=resid[:], in0=x_sb[b][:, r, :], in1=bias_all[:, 0:D], op=ALU.add)
-
-            o_t = psum_o.tile([P, PAIR, P], F32)
-            words = o_sb[b][:, r, :].bitcast(F32)
-            for u in range(PAIR):
-                nc.tensor.transpose(
-                    out=o_t[:, u, :], in_=words[:, u : D // PAIR : PAIR], identity=identity[:]
+        def project_heads(b):
+            adder = nc.vector if b < RESID_ON_VECTOR else nc.gpsimd
+            resid = batch.tile([P, R, D], F32)
+            for r in range(R):
+                adder.tensor_tensor(
+                    out=resid[:, r, :], in0=x_sb[b][:, r, :], in1=bias_all[:, 0:D], op=ALU.add
                 )
-            o_grouped = group.tile([P, P * PACK], BF16, align_bytes=64)
+
+            o_t = psum_o.tile([P, R, PAIR, P], F32)
+            for r in range(R):
+                words = o_sb[b][:, r, :].bitcast(F32)
+                for u in range(PAIR):
+                    nc.tensor.transpose(
+                        out=o_t[:, r, u, :], in_=words[:, u : D // PAIR : PAIR], identity=identity[:]
+                    )
+            o_grouped = work.tile([P, R * P * PACK], BF16, align_bytes=64)
             nc.scalar.copy(
-                out=o_grouped[:].bitcast(F32).rearrange("p (c u) -> p c u", u=PAIR),
-                in_=o_t[:].rearrange("p u c -> p c u"),
+                out=o_grouped[:].bitcast(F32).rearrange("p (r c u) -> p r c u", r=R, u=PAIR),
+                in_=o_t[:].rearrange("p r u c -> p r c u"),
             )
-            o_codes = group.tile([P, P], U32, align_bytes=64)
-            o_scales = group.tile([P, P], U8, align_bytes=64)
+            o_codes = work.tile([P, R * P], U32, align_bytes=64)
+            o_scales = work.tile([P, R * P], U8, align_bytes=64)
             nc.vector.quantize_mx(out=o_codes[:].bitcast(FP8X4), scales=o_scales[:], in_=o_grouped[:])
 
-            x_acc = psum_x.tile([P, D], F32)
-            nc.tensor.matmul_mx(
-                out=x_acc[:],
-                lhsT=o_codes[:].bitcast(FP8X4),
-                lhsT_scale=o_scales[:],
-                rhs=wo_words[:].bitcast(FP8X4),
-                rhs_scale=w_scales[:, 0:D],
-                start=True,
-                stop=True,
-            )
-            if r == 0:
-                x_loc_b = batch.tile([P, R, D], F32)
-                x_loc[b] = x_loc_b
-            token_sum = group.tile([P, 1], F32)
-            nc.vector.scalar_tensor_tensor(
-                out=x_loc[b][:, r, :],
-                in0=x_acc[:],
-                scalar=1.0,
-                in1=resid[:],
-                op0=ALU.mult,
-                op1=ALU.add,
-                accum_out=token_sum[:],
-            )
-            if r == R - 1:
-                nc.sync.dma_start(
-                    out=out_0[b].rearrange("(p r) k -> p (r k)", r=R),
-                    in_=x_loc[b][:].rearrange("p r k -> p (r k)"),
+            x_loc_b = batch.tile([P, R, D], F32)
+            token_sum = batch.tile([P, R], F32)
+            minus_mean_b = batch.tile([P, R], F32)
+            for r in range(R):
+                tokens = slice(r * P, (r + 1) * P)
+                x_acc = psum_x.tile([P, D], F32)
+                nc.tensor.matmul_mx(
+                    out=x_acc[:],
+                    lhsT=o_codes[:, tokens].bitcast(FP8X4),
+                    lhsT_scale=o_scales[:, tokens],
+                    rhs=wo_words[:].bitcast(FP8X4),
+                    rhs_scale=w_scales[:, 0:D],
+                    start=True,
+                    stop=True,
                 )
-            minus_mean_j = group.tile([P, 1], F32)
-            nc.scalar.mul(out=minus_mean_j[:], in_=token_sum[:], mul=-1.0 / D)
-            minus_mean[j] = minus_mean_j
+                nc.vector.scalar_tensor_tensor(
+                    out=x_loc_b[:, r, :],
+                    in0=x_acc[:],
+                    scalar=1.0,
+                    in1=resid[:, r, :],
+                    op0=ALU.mult,
+                    op1=ALU.add,
+                    accum_out=token_sum[:, r : r + 1],
+                )
+                nc.scalar.mul(
+                    out=minus_mean_b[:, r : r + 1], in_=token_sum[:, r : r + 1], mul=-1.0 / D
+                )
+            nc.sync.dma_start(
+                out=out_0[b].rearrange("(p r) k -> p (r k)", r=R),
+                in_=x_loc_b[:].rearrange("p r k -> p (r k)"),
+            )
+            x_loc[b] = x_loc_b
+            minus_mean[b] = minus_mean_b
 
-        def normalise(j):
-            b, r = divmod(j, R)
-            squares = group.tile([P, D], BF16)
-            sum_sq = group.tile([P, 1], F32)
-            nc.scalar.activation(
-                out=squares[:],
-                in_=x_loc[b][:, r, :],
-                func=ACT.Square,
-                bias=minus_mean[j][:],
-                scale=1.0,
-                accum_out=sum_sq[:],
-            )
-            var_eps = group.tile([P, 1], F32)
-            nc.gpsimd.tensor_scalar(
-                out=var_eps[:], in0=sum_sq[:], scalar1=1.0 / D, scalar2=EPS, op0=ALU.mult, op1=ALU.add
-            )
-            rstd = group.tile([P, 1], F32)
-            nc.gpsimd.tensor_tensor(out=rstd[:], in0=var_eps[:], in1=minus_half[:], op=ALU.pow)
-            normed_j = group.tile([P, PACK, P], F32)
-            nc.gpsimd.tensor_scalar(
-                out=normed_j[:],
-                in0=x_loc[b][:, r, :].rearrange("p (q t) -> p t q", t=PACK),
-                scalar1=minus_mean[j][:],
-                scalar2=rstd[:],
-                op0=ALU.add,
-                op1=ALU.mult,
-            )
-            normed[j] = normed_j
-
-        def quantise_h(j):
-            normed_t = psum_h.tile([P, PACK, P], F32)
-            for t in range(PACK):
-                nc.tensor.transpose(out=normed_t[:, t, :], in_=normed[j][:, t, :], identity=identity[:])
-            h_t = group.tile([P, PACK, P], BF16)
-            for t in range(PACK):
+        def normalise(b):
+            squares = work.tile([P, R, D], BF16)
+            sum_sq = batch.tile([P, R], F32)
+            var_eps = batch.tile([P, R], F32)
+            rstd = batch.tile([P, R], F32)
+            normed_b = work.tile([P, R, PACK, P], F32)
+            for r in range(R):
+                one = slice(r, r + 1)
                 nc.scalar.activation(
-                    out=h_t[:, t, :],
-                    in_=normed_t[:, t, :],
-                    func=ACT.Identity,
-                    scale=gain[:, t : t + 1],
-                    bias=shift[:, t : t + 1],
+                    out=squares[:, r, :],
+                    in_=x_loc[b][:, r, :],
+                    func=ACT.Square,
+                    bias=minus_mean[b][:, one],
+                    scale=1.0,
+                    accum_out=sum_sq[:, one],
                 )
-            h_grouped = group.tile([P, P, PACK], BF16, align_bytes=64)
+                nc.gpsimd.tensor_scalar(
+                    out=var_eps[:, one], in0=sum_sq[:, one], scalar1=1.0 / D, scalar2=EPS, op0=ALU.mult, op1=ALU.add
+                )
+                nc.gpsimd.tensor_tensor(out=rstd[:, one], in0=var_eps[:, one], in1=minus_half[:, one], op=ALU.pow)
+                nc.gpsimd.tensor_scalar(
+                    out=normed_b[:, r, :, :],
+                    in0=x_loc[b][:, r, :].rearrange("p (q t) -> p t q", t=PACK),
+                    scalar1=minus_mean[b][:, one],
+                    scalar2=rstd[:, one],
+                    op0=ALU.add,
+                    op1=ALU.mult,
+                )
+            normed[b] = normed_b
+
+        def quantise_h(b):
+            h_t = work.tile([P, PACK, R * P], BF16)
+            for half in range(PACK // 2):
+                normed_t = psum_h.tile([P, 2, R, P], F32)
+                for i in range(2):
+                    for r in range(R):
+                        nc.tensor.transpose(
+                            out=normed_t[:, i, r, :],
+                            in_=normed[b][:, r, 2 * half + i, :],
+                            identity=identity[:],
+                        )
+                for i in range(2):
+                    t = 2 * half + i
+                    nc.scalar.activation(
+                        out=h_t[:, t, :],
+                        in_=normed_t[:, i, :, :].rearrange("p r c -> p (r c)"),
+                        func=ACT.Identity,
+                        scale=gain[:, t : t + 1],
+                        bias=shift[:, t : t + 1],
+                    )
+            h_grouped = work.tile([P, R * P, PACK], BF16, align_bytes=64)
             nc.scalar.copy(out=h_grouped[:], in_=h_t[:].rearrange("p t c -> p c t"))
-            h_codes_j = group.tile([P, P], U32, align_bytes=64)
-            h_scales_j = group.tile([P, P], U8, align_bytes=64)
+            h_codes_b = work.tile([P, R * P], U32, align_bytes=64)
+            h_scales_b = work.tile([P, R * P], U8, align_bytes=64)
             nc.vector.quantize_mx(
-                out=h_codes_j[:].bitcast(FP8X4),
-                scales=h_scales_j[:],
+                out=h_codes_b[:].bitcast(FP8X4),
+                scales=h_scales_b[:],
                 in_=h_grouped[:].rearrange("p c t -> p (c t)"),
             )
-            h_codes[j] = h_codes_j
-            h_scales[j] = h_scales_j
+            h_codes[b] = h_codes_b
+            h_scales[b] = h_scales_b
 
         def project_qkv(b):
             for w in range(N_QKV):
                 cols = slice(D + w * D, D + (w + 1) * D)
                 head_rows = heads.tile([P, NH, R, HD], F32)
                 for r in range(R):
-                    j = R * b + r
+                    tokens = slice(r * P, (r + 1) * P)
                     qkv_acc = psum_qkv.tile([P, D], F32, tag="qkv_acc")
                     nc.tensor.matmul_mx(
                         out=qkv_acc[:],
-                        lhsT=h_codes[j][:].bitcast(FP8X4),
-                        lhsT_scale=h_scales[j][:],
+                        lhsT=h_codes[b][:, tokens].bitcast(FP8X4),
+                        lhsT_scale=h_scales[b][:, tokens],
                         rhs=wqkv_words[:, w * D : (w + 1) * D].bitcast(FP8X4),
                         rhs_scale=w_scales[:, cols],
                         start=True,
@@ -272,14 +286,11 @@ def tile_block_pa_kernel(
                 )
 
         spread_bias(bo_rows, 0)
-        for step in range(TILES + 8):
-            if step < TILES:
-                project_heads(step)
-            if step == 1:
+        stages = [project_heads, normalise, quantise_h, project_qkv]
+        for step in range(B + len(stages) - 1):
+            for i, stage in enumerate(stages):
+                b = step - i
+                if 0 <= b < B:
+                    stage(b)
+            if step == 0:
                 spread_bias(bqkv_rows, D)
-            if 0 <= step - 1 < TILES:
-                normalise(step - 1)
-            if 0 <= step - 2 < TILES:
-                quantise_h(step - 2)
-            if 0 <= step - 8 < TILES and (step - 8) % R == R - 1:
-                project_qkv((step - 8) // R)

@@ -48,12 +48,9 @@ def tile_block_pa_kernel(
     with ExitStack() as ctx:
         const = ctx.enter_context(tc.tile_pool(name="const", bufs=1))
         batch = ctx.enter_context(tc.tile_pool(name="batch", bufs=B))
-        work = ctx.enter_context(tc.tile_pool(name="work", bufs=2))
-        heads = ctx.enter_context(tc.tile_pool(name="heads", bufs=2 * N_QKV))
-        psum_o = ctx.enter_context(tc.psum_pool(name="psum_o", bufs=1))
-        psum_x = ctx.enter_context(tc.psum_pool(name="psum_x", bufs=2))
-        psum_h = ctx.enter_context(tc.psum_pool(name="psum_h", bufs=2))
-        psum_qkv = ctx.enter_context(tc.psum_pool(name="psum_qkv", bufs=3))
+        work = ctx.enter_context(tc.tile_pool(name="work", bufs=B))
+        heads = ctx.enter_context(tc.tile_pool(name="heads", bufs=B * N_QKV))
+        psum = ctx.enter_context(tc.psum_pool(name="psum", bufs=8))
 
         o_sb = {}
         x_sb = {}
@@ -116,7 +113,7 @@ def tile_block_pa_kernel(
 
         def spread_bias(rows, first_col):
             for j in range(rows.shape[1] // D):
-                spread = psum_qkv.tile([P, D], F32, tag="qkv_acc")
+                spread = psum.tile([P, D], F32, tag="bank")
                 nc.tensor.matmul(
                     out=spread[:], lhsT=ones[:], rhs=rows[:, j * D : (j + 1) * D], start=True, stop=True
                 )
@@ -146,7 +143,7 @@ def tile_block_pa_kernel(
                     out=resid[:, r, :], in0=x_sb[b][:, r, :], in1=bias_all[:, 0:D], op=ALU.add
                 )
 
-            o_t = psum_o.tile([P, R, PAIR, P], F32)
+            o_t = psum.tile([P, R, PAIR, P], F32, tag="bank")
             for r in range(R):
                 words = o_sb[b][:, r, :].bitcast(F32)
                 for u in range(PAIR):
@@ -167,7 +164,7 @@ def tile_block_pa_kernel(
             minus_mean_b = batch.tile([P, R], F32)
             for r in range(R):
                 tokens = slice(r * P, (r + 1) * P)
-                x_acc = psum_x.tile([P, D], F32)
+                x_acc = psum.tile([P, D], F32, tag="bank")
                 nc.tensor.matmul_mx(
                     out=x_acc[:],
                     lhsT=o_codes[:, tokens].bitcast(FP8X4),
@@ -229,7 +226,7 @@ def tile_block_pa_kernel(
         def quantise_h(b):
             h_t = work.tile([P, PACK, R * P], BF16)
             for half in range(PACK // 2):
-                normed_t = psum_h.tile([P, 2, R, P], F32)
+                normed_t = psum.tile([P, 2, R, P], F32, tag="bank")
                 for i in range(2):
                     for r in range(R):
                         nc.tensor.transpose(
@@ -264,7 +261,7 @@ def tile_block_pa_kernel(
                 head_rows = heads.tile([P, NH, R, HD], F32)
                 for r in range(R):
                     tokens = slice(r * P, (r + 1) * P)
-                    qkv_acc = psum_qkv.tile([P, D], F32, tag="qkv_acc")
+                    qkv_acc = psum.tile([P, D], F32, tag="bank")
                     nc.tensor.matmul_mx(
                         out=qkv_acc[:],
                         lhsT=h_codes[b][:, tokens].bitcast(FP8X4),

@@ -21,7 +21,8 @@ N_QKV = 3
 N_ALL = D + N_QKV * D
 BLOCK_ROWS = 16
 EPS = 1e-5
-RESID_ON_VECTOR = 4
+RESID_ON_VECTOR = (0,)
+REGROUP_ON_VECTOR = (0,)
 FLOPS = 2 * B * S * D * N_ALL
 
 
@@ -46,248 +47,367 @@ def tile_block_pa_kernel(
     qkv_out = [out_1, out_2, out_3]
 
     with ExitStack() as ctx:
+        ctx.enter_context(tc.manual_schedule())
         const = ctx.enter_context(tc.tile_pool(name="const", bufs=1))
         batch = ctx.enter_context(tc.tile_pool(name="batch", bufs=B))
-        work = ctx.enter_context(tc.tile_pool(name="work", bufs=B))
+        work = ctx.enter_context(tc.tile_pool(name="work", bufs=B * R))
         heads = ctx.enter_context(tc.tile_pool(name="heads", bufs=B * N_QKV))
         psum = ctx.enter_context(tc.psum_pool(name="psum", bufs=8))
 
         o_sb = {}
         x_sb = {}
 
-        def load_batch(b):
+        def load_o(b):
             o_b = batch.tile([P, R, D], BF16)
             by_r = o_loc[b].rearrange("n (p r) d -> r p n d", r=R)
             for r in range(R):
                 nc.sync.dma_start(out=o_b[:, r, :].rearrange("p (n d) -> p n d", n=NH), in_=by_r[r])
+            o_sb[b] = o_b
+
+        def load_x(b):
             x_b = batch.tile([P, R, D], BF16)
             nc.sync.dma_start(
                 out=x_b[:].rearrange("p r k -> p (r k)"),
                 in_=x[b].rearrange("(p r) k -> p (r k)", r=R),
             )
-            o_sb[b] = o_b
             x_sb[b] = x_b
 
-        w_scales = const.tile([P, N_ALL], U8, align_bytes=64)
-        nc.vector.memset(w_scales[:].bitcast(I32), 0)
+        wo_scales = const.tile([P, D], U8, align_bytes=64)
+        nc.vector.memset(wo_scales[:].bitcast(I32), 0)
+        bo_rows = const.tile([P, D], BF16)
+        nc.vector.memset(bo_rows[:], 0.0)
+        ones = const.tile([P, P], BF16)
+        nc.vector.memset(ones[:], 1.0)
+        wqkv_scales = const.tile([P, N_QKV * D], U8, align_bytes=64)
+        nc.vector.memset(wqkv_scales[:].bitcast(I32), 0)
+        bqkv_rows = const.tile([P, N_QKV * D], BF16)
+        nc.vector.memset(bqkv_rows[:], 0.0)
 
-        def load_scales(rows, cols):
+        def load_scales(scales, rows):
             for j in range(4):
                 nc.sync.dma_start(
-                    out=w_scales[j:P:32, cols].bitcast(I32),
+                    out=scales[j:P:32, :].bitcast(I32),
                     in_=rows[j:BLOCK_ROWS:4, :].bitcast(I32),
                 )
 
         wo_words = const.tile([P, D], U32, align_bytes=64)
         wqkv_words = const.tile([P, N_QKV * D], U32, align_bytes=64)
 
-        bo_rows = const.tile([P, D], BF16)
-        nc.vector.memset(bo_rows[:], 0.0)
-        ones = const.tile([P, P], BF16)
-        nc.vector.memset(ones[:], 1.0)
-        bqkv_rows = const.tile([P, N_QKV * D], BF16)
-        nc.vector.memset(bqkv_rows[:], 0.0)
-        gain_bf = const.tile([P, PACK], BF16)
-        shift_bf = const.tile([P, PACK], BF16)
-
-        load_scales(Wo_l_scales[0], slice(0, D))
+        load_scales(wo_scales, Wo_l_scales[0])
         nc.sync.dma_start(out=bo_rows[0:1, :], in_=bo_l.rearrange("(o n) -> o n", o=1))
+        load_o(0)
         nc.sync.dma_start(
             out=wo_words[:].bitcast(I32),
             in_=Wo_l_words[0].rearrange("p n t -> p (n t)").bitcast(I32),
         )
-        load_batch(0)
-        nc.sync.dma_start(out=gain_bf[:], in_=ln2_w.rearrange("(p t) -> p t", t=PACK))
-        nc.sync.dma_start(out=shift_bf[:], in_=ln2_b.rearrange("(p t) -> p t", t=PACK))
-        load_batch(1)
+        load_x(0)
+        load_o(1)
+        load_x(1)
         nc.sync.dma_start(out=bqkv_rows[0:1, :], in_=bqkv_g.rearrange("(o n) -> o n", o=1))
-        load_scales(Wqkv_g_scales[0], slice(D, N_ALL))
+        load_o(2)
+        load_x(2)
+        load_scales(wqkv_scales, Wqkv_g_scales[0])
         nc.sync.dma_start(
             out=wqkv_words[:].bitcast(I32),
             in_=Wqkv_g_words[0].rearrange("p n t -> p (n t)").bitcast(I32),
         )
-        load_batch(2)
-        load_batch(3)
-
-        bias_all = const.tile([P, N_ALL], F32)
-
-        def spread_bias(rows, first_col):
-            for j in range(rows.shape[1] // D):
-                spread = psum.tile([P, D], F32, tag="bank")
-                nc.tensor.matmul(
-                    out=spread[:], lhsT=ones[:], rhs=rows[:, j * D : (j + 1) * D], start=True, stop=True
-                )
-                nc.scalar.copy(out=bias_all[:, first_col + j * D : first_col + (j + 1) * D], in_=spread[:])
-
-        gain = const.tile([P, PACK], F32)
-        shift = const.tile([P, PACK], F32)
-        nc.gpsimd.tensor_copy(out=gain[:], in_=gain_bf[:])
-        nc.gpsimd.tensor_copy(out=shift[:], in_=shift_bf[:])
+        load_o(3)
+        load_x(3)
 
         identity = const.tile([P, P], F32)
         masks.make_identity(nc, identity[:])
-        minus_half = const.tile([P, R], F32)
-        nc.vector.memset(minus_half[:], -0.5)
+        gain_bf = const.tile([P, PACK], BF16)
+        shift_bf = const.tile([P, PACK], BF16)
+        nc.gpsimd.dma_start(out=gain_bf[:], in_=ln2_w.rearrange("(p t) -> p t", t=PACK))
+        nc.gpsimd.dma_start(out=shift_bf[:], in_=ln2_b.rearrange("(p t) -> p t", t=PACK))
+        gain = const.tile([P, PACK], F32)
+        shift = const.tile([P, PACK], F32)
 
+        def widen_affine():
+            nc.gpsimd.tensor_copy(out=gain[:], in_=gain_bf[:])
+            nc.gpsimd.tensor_copy(out=shift[:], in_=shift_bf[:])
+
+        table = const.tile([P, 1], F32)
+        nc.scalar.activation(
+            out=table[:], in_=ones[:, 0:1], func=ACT.Abs_reciprocal_sqrt, bias=EPS, scale=1.0 / D
+        )
+
+        bias_all = const.tile([P, N_ALL], F32)
+
+        spread = {}
+
+        def spread_bias(i, rows):
+            spread[i] = psum.tile([P, D], F32, tag="bank", name="spread_i")
+            nc.tensor.matmul(out=spread[i][:], lhsT=ones[:], rhs=rows, start=True, stop=True)
+
+        def copy_bias(i, copy):
+            copy(out=bias_all[:, i * D : (i + 1) * D], in_=spread[i][:])
+
+        resid = {}
+        o_grouped = {}
+        o_codes = {}
+        o_scales = {}
         x_loc = {}
+        x_accs = {}
         minus_mean = {}
         normed = {}
+        h_t = {}
+        h_grouped = {}
         h_codes = {}
         h_scales = {}
 
-        def project_heads(b):
-            adder = nc.vector if b < RESID_ON_VECTOR else nc.gpsimd
-            resid = batch.tile([P, R, D], F32)
-            for r in range(R):
-                adder.tensor_tensor(
-                    out=resid[:, r, :], in0=x_sb[b][:, r, :], in1=bias_all[:, 0:D], op=ALU.add
-                )
+        def add_resid(b, r):
+            adder = nc.vector if b in RESID_ON_VECTOR else nc.gpsimd
+            resid[b, r] = work.tile([P, D], F32, name="resid_b")
+            adder.tensor_tensor(
+                out=resid[b, r][:], in0=x_sb[b][:, r, :], in1=bias_all[:, 0:D], op=ALU.add
+            )
 
-            o_t = psum.tile([P, R, PAIR, P], F32, tag="bank")
+        o_turned = {}
+
+        def turn_o(b):
+            o_turned[b] = psum.tile([P, R, PAIR, P], F32, tag="bank", name="o_turned_b")
             for r in range(R):
                 words = o_sb[b][:, r, :].bitcast(F32)
                 for u in range(PAIR):
                     nc.tensor.transpose(
-                        out=o_t[:, r, u, :], in_=words[:, u : D // PAIR : PAIR], identity=identity[:]
+                        out=o_turned[b][:, r, u, :], in_=words[:, u : D // PAIR : PAIR], identity=identity[:]
                     )
-            o_grouped = work.tile([P, R * P * PACK], BF16, align_bytes=64)
-            nc.scalar.copy(
-                out=o_grouped[:].bitcast(F32).rearrange("p (r c u) -> p r c u", r=R, u=PAIR),
-                in_=o_t[:].rearrange("p r u c -> p r c u"),
-            )
-            o_codes = work.tile([P, R * P], U32, align_bytes=64)
-            o_scales = work.tile([P, R * P], U8, align_bytes=64)
-            nc.vector.quantize_mx(out=o_codes[:].bitcast(FP8X4), scales=o_scales[:], in_=o_grouped[:])
 
-            x_loc_b = batch.tile([P, R, D], F32)
-            token_sum = batch.tile([P, R], F32)
-            minus_mean_b = batch.tile([P, R], F32)
+        def group_o(b):
+            o_grouped[b] = work.tile([P, R * P * PACK], BF16, align_bytes=64, name="o_grouped_b")
+            nc.scalar.copy(
+                out=o_grouped[b][:].bitcast(F32).rearrange("p (r c u) -> p r c u", r=R, u=PAIR),
+                in_=o_turned[b][:].rearrange("p r u c -> p r c u"),
+            )
+
+        def quantise_o(b):
+            o_codes[b] = work.tile([P, R * P], U32, align_bytes=64, name="o_codes_b")
+            o_scales[b] = work.tile([P, R * P], U8, align_bytes=64, name="o_scales_b")
+            nc.vector.quantize_mx(
+                out=o_codes[b][:].bitcast(FP8X4), scales=o_scales[b][:], in_=o_grouped[b][:]
+            )
+
+        def project_o(b):
+            x_accs[b] = []
             for r in range(R):
                 tokens = slice(r * P, (r + 1) * P)
                 x_acc = psum.tile([P, D], F32, tag="bank")
                 nc.tensor.matmul_mx(
                     out=x_acc[:],
-                    lhsT=o_codes[:, tokens].bitcast(FP8X4),
-                    lhsT_scale=o_scales[:, tokens],
+                    lhsT=o_codes[b][:, tokens].bitcast(FP8X4),
+                    lhsT_scale=o_scales[b][:, tokens],
                     rhs=wo_words[:].bitcast(FP8X4),
-                    rhs_scale=w_scales[:, 0:D],
+                    rhs_scale=wo_scales[:],
                     start=True,
                     stop=True,
                 )
+                x_accs[b].append(x_acc)
+
+        token_sums = {}
+
+        def finish_x_loc(b):
+            x_loc[b] = batch.tile([P, R, D], F32, name="x_loc_b")
+            for r in range(R):
+                token_sums[b, r] = work.tile([P, 1], F32, name="token_sum_b")
                 nc.vector.scalar_tensor_tensor(
-                    out=x_loc_b[:, r, :],
-                    in0=x_acc[:],
+                    out=x_loc[b][:, r, :],
+                    in0=x_accs[b][r][:],
                     scalar=1.0,
-                    in1=resid[:, r, :],
+                    in1=resid[b, r][:],
                     op0=ALU.mult,
                     op1=ALU.add,
-                    accum_out=token_sum[:, r : r + 1],
-                )
-                nc.scalar.mul(
-                    out=minus_mean_b[:, r : r + 1], in_=token_sum[:, r : r + 1], mul=-1.0 / D
+                    accum_out=token_sums[b, r][:],
                 )
             nc.sync.dma_start(
                 out=out_0[b].rearrange("(p r) k -> p (r k)", r=R),
-                in_=x_loc_b[:].rearrange("p r k -> p (r k)"),
+                in_=x_loc[b][:].rearrange("p r k -> p (r k)"),
             )
-            x_loc[b] = x_loc_b
-            minus_mean[b] = minus_mean_b
 
-        def normalise(b):
-            squares = work.tile([P, R, D], BF16)
-            sum_sq = batch.tile([P, R], F32)
-            var_eps = batch.tile([P, R], F32)
-            rstd = batch.tile([P, R], F32)
-            normed_b = work.tile([P, R, PACK, P], F32)
-            for r in range(R):
-                one = slice(r, r + 1)
+        def normalise(b, r):
+            minus_mean = work.tile([P, 1], F32)
+            squares = work.tile([P, D], BF16)
+            sum_sq = work.tile([P, 1], F32)
+            rstd = work.tile([P, 1], F32)
+            nc.scalar.mul(out=minus_mean[:], in_=token_sums[b, r][:], mul=-1.0 / D)
+            nc.scalar.activation(
+                out=squares[:],
+                in_=x_loc[b][:, r, :],
+                func=ACT.Square,
+                bias=minus_mean[:],
+                scale=1.0,
+                accum_out=sum_sq[:],
+            )
+            nc.scalar.activation(
+                out=rstd[:], in_=sum_sq[:], func=ACT.Abs_reciprocal_sqrt, bias=EPS, scale=1.0 / D
+            )
+            normed[b, r] = work.tile([P, PACK, P], F32, name="normed_b")
+            nc.gpsimd.tensor_scalar(
+                out=normed[b, r][:],
+                in0=x_loc[b][:, r, :].rearrange("p (q t) -> p t q", t=PACK),
+                scalar1=minus_mean[:],
+                scalar2=rstd[:],
+                op0=ALU.add,
+                op1=ALU.mult,
+            )
+
+        normed_turned = {}
+
+        def turn_h(b, r):
+            normed_turned[b, r] = psum.tile([P, PACK, P], F32, tag="bank", name="normed_turned_b")
+            for t in range(PACK):
+                nc.tensor.transpose(
+                    out=normed_turned[b, r][:, t, :], in_=normed[b, r][:, t, :], identity=identity[:]
+                )
+
+        def scale_h(b, r):
+            h_t[b, r] = work.tile([P, PACK, P], BF16, name="h_t_b")
+            for t in range(PACK):
                 nc.scalar.activation(
-                    out=squares[:, r, :],
-                    in_=x_loc[b][:, r, :],
-                    func=ACT.Square,
-                    bias=minus_mean[b][:, one],
-                    scale=1.0,
-                    accum_out=sum_sq[:, one],
+                    out=h_t[b, r][:, t, :],
+                    in_=normed_turned[b, r][:, t, :],
+                    func=ACT.Identity,
+                    scale=gain[:, t : t + 1],
+                    bias=shift[:, t : t + 1],
                 )
-                nc.gpsimd.tensor_scalar(
-                    out=var_eps[:, one], in0=sum_sq[:, one], scalar1=1.0 / D, scalar2=EPS, op0=ALU.mult, op1=ALU.add
-                )
-                nc.gpsimd.tensor_tensor(out=rstd[:, one], in0=var_eps[:, one], in1=minus_half[:, one], op=ALU.pow)
-                nc.gpsimd.tensor_scalar(
-                    out=normed_b[:, r, :, :],
-                    in0=x_loc[b][:, r, :].rearrange("p (q t) -> p t q", t=PACK),
-                    scalar1=minus_mean[b][:, one],
-                    scalar2=rstd[:, one],
-                    op0=ALU.add,
-                    op1=ALU.mult,
-                )
-            normed[b] = normed_b
 
-        def quantise_h(b):
-            h_t = work.tile([P, PACK, R * P], BF16)
-            for half in range(PACK // 2):
-                normed_t = psum.tile([P, 2, R, P], F32, tag="bank")
-                for i in range(2):
-                    for r in range(R):
-                        nc.tensor.transpose(
-                            out=normed_t[:, i, r, :],
-                            in_=normed[b][:, r, 2 * half + i, :],
-                            identity=identity[:],
-                        )
-                for i in range(2):
-                    t = 2 * half + i
-                    nc.scalar.activation(
-                        out=h_t[:, t, :],
-                        in_=normed_t[:, i, :, :].rearrange("p r c -> p (r c)"),
-                        func=ACT.Identity,
-                        scale=gain[:, t : t + 1],
-                        bias=shift[:, t : t + 1],
-                    )
-            h_grouped = work.tile([P, R * P, PACK], BF16, align_bytes=64)
-            nc.scalar.copy(out=h_grouped[:], in_=h_t[:].rearrange("p t c -> p c t"))
-            h_codes_b = work.tile([P, R * P], U32, align_bytes=64)
-            h_scales_b = work.tile([P, R * P], U8, align_bytes=64)
+        def group_h(b, r):
+            h_grouped[b, r] = work.tile([P, P, PACK], BF16, align_bytes=64, name="h_grouped_b")
+            copy = nc.vector.tensor_copy if b in REGROUP_ON_VECTOR else nc.scalar.copy
+            copy(out=h_grouped[b, r][:], in_=h_t[b, r][:].rearrange("p t c -> p c t"))
+
+        def quantise_h(b, r):
+            h_codes[b, r] = work.tile([P, P], U32, align_bytes=64, name="h_codes_b")
+            h_scales[b, r] = work.tile([P, P], U8, align_bytes=64, name="h_scales_b")
             nc.vector.quantize_mx(
-                out=h_codes_b[:].bitcast(FP8X4),
-                scales=h_scales_b[:],
-                in_=h_grouped[:].rearrange("p c t -> p (c t)"),
+                out=h_codes[b, r][:].bitcast(FP8X4),
+                scales=h_scales[b, r][:],
+                in_=h_grouped[b, r][:].rearrange("p c t -> p (c t)"),
             )
-            h_codes[b] = h_codes_b
-            h_scales[b] = h_scales_b
 
-        def project_qkv(b):
+        qkv_accs = {}
+        head_rows = {}
+
+        def project_qkv(b, r):
+            for w in range(N_QKV):
+                qkv_accs[b, r, w] = psum.tile([P, D], F32, tag="bank", name="qkv_acc")
+                nc.tensor.matmul_mx(
+                    out=qkv_accs[b, r, w][:],
+                    lhsT=h_codes[b, r][:].bitcast(FP8X4),
+                    lhsT_scale=h_scales[b, r][:],
+                    rhs=wqkv_words[:, w * D : (w + 1) * D].bitcast(FP8X4),
+                    rhs_scale=wqkv_scales[:, w * D : (w + 1) * D],
+                    start=True,
+                    stop=True,
+                )
+
+        def finish_qkv(b, r):
             for w in range(N_QKV):
                 cols = slice(D + w * D, D + (w + 1) * D)
-                head_rows = heads.tile([P, NH, R, HD], F32)
-                for r in range(R):
-                    tokens = slice(r * P, (r + 1) * P)
-                    qkv_acc = psum.tile([P, D], F32, tag="bank")
-                    nc.tensor.matmul_mx(
-                        out=qkv_acc[:],
-                        lhsT=h_codes[b][:, tokens].bitcast(FP8X4),
-                        lhsT_scale=h_scales[b][:, tokens],
-                        rhs=wqkv_words[:, w * D : (w + 1) * D].bitcast(FP8X4),
-                        rhs_scale=w_scales[:, cols],
-                        start=True,
-                        stop=True,
-                    )
-                    nc.vector.tensor_tensor(
-                        out=head_rows[:, :, r, :],
-                        in0=qkv_acc[:].rearrange("p (n d) -> p n d", n=NH),
-                        in1=bias_all[:, cols].rearrange("p (n d) -> p n d", n=NH),
-                        op=ALU.add,
-                    )
-                nc.sync.dma_start(
-                    out=qkv_out[w][b].rearrange("n (p r) d -> p n (r d)", r=R),
-                    in_=head_rows[:].rearrange("p n r d -> p n (r d)"),
+                if r == 0:
+                    head_rows[b, w] = heads.tile([P, NH, R, HD], F32, name="head_rows_b")
+                nc.vector.tensor_tensor(
+                    out=head_rows[b, w][:, :, r, :],
+                    in0=qkv_accs[b, r, w][:].rearrange("p (n d) -> p n d", n=NH),
+                    in1=bias_all[:, cols].rearrange("p (n d) -> p n d", n=NH),
+                    op=ALU.add,
                 )
+                if r == R - 1:
+                    nc.sync.dma_start(
+                        out=qkv_out[w][b].rearrange("n (p r) d -> p n (r d)", r=R),
+                        in_=head_rows[b, w][:].rearrange("p n r d -> p n (r d)"),
+                    )
 
-        spread_bias(bo_rows, 0)
-        stages = [project_heads, normalise, quantise_h, project_qkv]
-        for step in range(B + len(stages) - 1):
-            for i, stage in enumerate(stages):
-                b = step - i
-                if 0 <= b < B:
-                    stage(b)
-            if step == 0:
-                spread_bias(bqkv_rows, D)
+        spread_bias(0, bo_rows[:])
+        copy_bias(0, nc.vector.tensor_copy)
+        turn_o(0)
+        add_resid(1, 0)
+        add_resid(1, 1)
+        add_resid(2, 0)
+        widen_affine()
+        turn_o(1)
+        group_o(0)
+        add_resid(0, 0)
+        add_resid(0, 1)
+        quantise_o(0)
+        project_o(0)
+        group_o(1)
+        spread_bias(1, bqkv_rows[:, 0 * D : 1 * D])
+        spread_bias(2, bqkv_rows[:, 1 * D : 2 * D])
+        spread_bias(3, bqkv_rows[:, 2 * D : 3 * D])
+        finish_x_loc(0)
+        quantise_o(1)
+        copy_bias(1, nc.vector.tensor_copy)
+        project_o(1)
+        turn_o(2)
+        normalise(0, 0)
+        normalise(0, 1)
+        group_o(2)
+        finish_x_loc(1)
+        copy_bias(2, nc.vector.tensor_copy)
+        turn_h(0, 0)
+        scale_h(0, 0)
+        turn_h(0, 1)
+        turn_o(3)
+        scale_h(0, 1)
+        quantise_o(2)
+        project_o(2)
+        group_h(0, 0)
+        quantise_h(0, 0)
+        copy_bias(3, nc.vector.tensor_copy)
+        project_qkv(0, 0)
+        group_h(0, 1)
+        quantise_h(0, 1)
+        project_qkv(0, 1)
+        group_o(3)
+        add_resid(2, 1)
+        normalise(1, 0)
+        normalise(1, 1)
+        finish_qkv(0, 0)
+        finish_x_loc(2)
+        quantise_o(3)
+        add_resid(3, 0)
+        add_resid(3, 1)
+        finish_qkv(0, 1)
+        turn_h(1, 0)
+        turn_h(1, 1)
+        scale_h(1, 0)
+        group_h(1, 0)
+        scale_h(1, 1)
+        group_h(1, 1)
+        project_o(3)
+        finish_x_loc(3)
+        normalise(2, 0)
+        normalise(2, 1)
+        quantise_h(1, 0)
+        quantise_h(1, 1)
+        project_qkv(1, 0)
+        turn_h(2, 0)
+        project_qkv(1, 1)
+        turn_h(2, 1)
+        normalise(3, 0)
+        scale_h(2, 0)
+        group_h(2, 0)
+        normalise(3, 1)
+        scale_h(2, 1)
+        group_h(2, 1)
+        finish_qkv(1, 0)
+        finish_qkv(1, 1)
+        quantise_h(2, 0)
+        quantise_h(2, 1)
+        project_qkv(2, 0)
+        turn_h(3, 0)
+        project_qkv(2, 1)
+        turn_h(3, 1)
+        scale_h(3, 0)
+        group_h(3, 0)
+        scale_h(3, 1)
+        group_h(3, 1)
+        finish_qkv(2, 0)
+        quantise_h(3, 0)
+        finish_qkv(2, 1)
+        quantise_h(3, 1)
+        project_qkv(3, 0)
+        project_qkv(3, 1)
+        finish_qkv(3, 0)
+        finish_qkv(3, 1)

@@ -208,8 +208,8 @@ def tile_block_pa_kernel(
 
         def finish_x_loc(b):
             x_loc[b] = batch.tile([P, R, D], F32, name="x_loc_b")
+            token_sums[b] = batch.tile([P, R], F32, name="token_sums_b")
             for r in range(R):
-                token_sums[b, r] = work.tile([P, 1], F32, name="token_sum_b")
                 nc.vector.scalar_tensor_tensor(
                     out=x_loc[b][:, r, :],
                     in0=x_accs[b][r][:],
@@ -217,39 +217,44 @@ def tile_block_pa_kernel(
                     in1=resid[b, r][:],
                     op0=ALU.mult,
                     op1=ALU.add,
-                    accum_out=token_sums[b, r][:],
+                    accum_out=token_sums[b][:, r : r + 1],
                 )
             nc.sync.dma_start(
                 out=out_0[b].rearrange("(p r) k -> p (r k)", r=R),
                 in_=x_loc[b][:].rearrange("p r k -> p (r k)"),
             )
 
-        def normalise(b, r):
-            minus_mean = work.tile([P, 1], F32)
-            squares = work.tile([P, D], BF16)
-            sum_sq = work.tile([P, 1], F32)
-            rstd = work.tile([P, 1], F32)
-            nc.scalar.mul(out=minus_mean[:], in_=token_sums[b, r][:], mul=-1.0 / D)
-            nc.scalar.activation(
-                out=squares[:],
-                in_=x_loc[b][:, r, :],
-                func=ACT.Square,
-                bias=minus_mean[:],
-                scale=1.0,
-                accum_out=sum_sq[:],
+        def normalise(b, tokens=range(R)):
+            n = len(tokens)
+            minus_mean = work.tile([P, n], F32)
+            sum_sq = work.tile([P, n], F32)
+            rstd = work.tile([P, n], F32)
+            nc.scalar.mul(
+                out=minus_mean[:], in_=token_sums[b][:, tokens[0] : tokens[0] + n], mul=-1.0 / D
             )
+            for i in range(n):
+                squares = work.tile([P, D], BF16)
+                nc.scalar.activation(
+                    out=squares[:],
+                    in_=x_loc[b][:, tokens[i], :],
+                    func=ACT.Square,
+                    bias=minus_mean[:, i : i + 1],
+                    scale=1.0,
+                    accum_out=sum_sq[:, i : i + 1],
+                )
             nc.scalar.activation(
                 out=rstd[:], in_=sum_sq[:], func=ACT.Abs_reciprocal_sqrt, bias=EPS, scale=1.0 / D
             )
-            normed[b, r] = work.tile([P, PACK, P], F32, name="normed_b")
-            nc.gpsimd.tensor_scalar(
-                out=normed[b, r][:],
-                in0=x_loc[b][:, r, :].rearrange("p (q t) -> p t q", t=PACK),
-                scalar1=minus_mean[:],
-                scalar2=rstd[:],
-                op0=ALU.add,
-                op1=ALU.mult,
-            )
+            for i in range(n):
+                normed[b, tokens[i]] = work.tile([P, PACK, P], F32, name="normed_b")
+                nc.gpsimd.tensor_scalar(
+                    out=normed[b, tokens[i]][:],
+                    in0=x_loc[b][:, tokens[i], :].rearrange("p (q t) -> p t q", t=PACK),
+                    scalar1=minus_mean[:, i : i + 1],
+                    scalar2=rstd[:, i : i + 1],
+                    op0=ALU.add,
+                    op1=ALU.mult,
+                )
 
         normed_turned = {}
 
@@ -288,8 +293,8 @@ def tile_block_pa_kernel(
         qkv_accs = {}
         head_rows = {}
 
-        def project_qkv(b, r):
-            for w in range(N_QKV):
+        def project_qkv(b, r, thirds=range(N_QKV)):
+            for w in thirds:
                 qkv_accs[b, r, w] = psum.tile([P, D], F32, tag="bank", name="qkv_acc")
                 nc.tensor.matmul_mx(
                     out=qkv_accs[b, r, w][:],
@@ -301,8 +306,8 @@ def tile_block_pa_kernel(
                     stop=True,
                 )
 
-        def finish_qkv(b, r):
-            for w in range(N_QKV):
+        def finish_qkv(b, r, thirds=range(N_QKV)):
+            for w in thirds:
                 cols = slice(D + w * D, D + (w + 1) * D)
                 if r == 0:
                     head_rows[b, w] = heads.tile([P, NH, R, HD], F32, name="head_rows_b")
@@ -340,74 +345,79 @@ def tile_block_pa_kernel(
         copy_bias(1, nc.vector.tensor_copy)
         project_o(1)
         turn_o(2)
-        normalise(0, 0)
-        normalise(0, 1)
+        normalise(0, [0])
+        normalise(0, [1])
         group_o(2)
         finish_x_loc(1)
         copy_bias(2, nc.vector.tensor_copy)
+        copy_bias(3, nc.vector.tensor_copy)
+        quantise_o(2)
         turn_h(0, 0)
         scale_h(0, 0)
         turn_h(0, 1)
-        turn_o(3)
-        scale_h(0, 1)
-        quantise_o(2)
         project_o(2)
+        scale_h(0, 1)
         group_h(0, 0)
         quantise_h(0, 0)
-        copy_bias(3, nc.vector.tensor_copy)
         project_qkv(0, 0)
+        turn_o(3)
+        add_resid(2, 1)
+        finish_x_loc(2)
         group_h(0, 1)
         quantise_h(0, 1)
         project_qkv(0, 1)
+        normalise(1)
         group_o(3)
-        add_resid(2, 1)
-        normalise(1, 0)
-        normalise(1, 1)
         finish_qkv(0, 0)
-        finish_x_loc(2)
         quantise_o(3)
         add_resid(3, 0)
         add_resid(3, 1)
-        finish_qkv(0, 1)
+        normalise(2)
         turn_h(1, 0)
         turn_h(1, 1)
+        project_o(3)
+        finish_qkv(0, 1)
         scale_h(1, 0)
         group_h(1, 0)
         scale_h(1, 1)
         group_h(1, 1)
-        project_o(3)
         finish_x_loc(3)
-        normalise(2, 0)
-        normalise(2, 1)
         quantise_h(1, 0)
-        quantise_h(1, 1)
         project_qkv(1, 0)
+        quantise_h(1, 1)
         turn_h(2, 0)
-        project_qkv(1, 1)
         turn_h(2, 1)
-        normalise(3, 0)
+        project_qkv(1, 1)
+        normalise(3)
         scale_h(2, 0)
         group_h(2, 0)
-        normalise(3, 1)
         scale_h(2, 1)
         group_h(2, 1)
         finish_qkv(1, 0)
-        finish_qkv(1, 1)
+        finish_qkv(1, 1, [0])
+        finish_qkv(1, 1, [1])
         quantise_h(2, 0)
-        quantise_h(2, 1)
         project_qkv(2, 0)
+        finish_qkv(1, 1, [2])
+        finish_qkv(2, 0, [0])
+        finish_qkv(2, 0, [1])
         turn_h(3, 0)
-        project_qkv(2, 1)
         turn_h(3, 1)
+        quantise_h(2, 1)
+        project_qkv(2, 1)
         scale_h(3, 0)
         group_h(3, 0)
         scale_h(3, 1)
         group_h(3, 1)
-        finish_qkv(2, 0)
+        finish_qkv(2, 0, [2])
+        finish_qkv(2, 1, [0])
+        finish_qkv(2, 1, [1])
         quantise_h(3, 0)
-        finish_qkv(2, 1)
-        quantise_h(3, 1)
         project_qkv(3, 0)
+        finish_qkv(2, 1, [2])
+        finish_qkv(3, 0, [0])
+        finish_qkv(3, 0, [1])
+        quantise_h(3, 1)
         project_qkv(3, 1)
-        finish_qkv(3, 0)
+        finish_qkv(3, 0, [2])
         finish_qkv(3, 1)

@@ -80,8 +80,7 @@ def tile_block_pa_kernel(
         nc.vector.memset(ones[:], 1.0)
         wqkv_scales = const.tile([P, N_QKV * D], U8, align_bytes=64)
         nc.vector.memset(wqkv_scales[:].bitcast(I32), 0)
-        bqkv_rows = const.tile([P, N_QKV * D], BF16)
-        nc.vector.memset(bqkv_rows[:], 0.0)
+        bqkv = const.tile([P, N_QKV * D], BF16)
 
         def load_scales(scales, rows):
             for j in range(4):
@@ -103,7 +102,6 @@ def tile_block_pa_kernel(
         load_x(0)
         load_o(1)
         load_x(1)
-        nc.sync.dma_start(out=bqkv_rows[0:1, :], in_=bqkv_g.rearrange("(o n) -> o n", o=1))
         load_o(2)
         load_x(2)
         load_scales(wqkv_scales, Wqkv_g_scales[0])
@@ -113,6 +111,7 @@ def tile_block_pa_kernel(
         )
         load_o(3)
         load_x(3)
+        nc.sync.dma_start(out=bqkv[:], in_=bqkv_g.partition_broadcast(P))
 
         identity = const.tile([P, P], F32)
         masks.make_identity(nc, identity[:])
@@ -132,16 +131,12 @@ def tile_block_pa_kernel(
             out=table[:], in_=ones[:, 0:1], func=ACT.Abs_reciprocal_sqrt, bias=EPS, scale=1.0 / D
         )
 
-        bias_all = const.tile([P, N_ALL], F32)
+        bo = const.tile([P, D], F32)
 
-        spread = {}
-
-        def spread_bias(i, rows):
-            spread[i] = psum.tile([P, D], F32, tag="bank", name="spread_i")
-            nc.tensor.matmul(out=spread[i][:], lhsT=ones[:], rhs=rows, start=True, stop=True)
-
-        def copy_bias(i, copy):
-            copy(out=bias_all[:, i * D : (i + 1) * D], in_=spread[i][:])
+        def spread_bo():
+            bo_spread = psum.tile([P, D], F32, tag="bank")
+            nc.tensor.matmul(out=bo_spread[:], lhsT=ones[:], rhs=bo_rows[:], start=True, stop=True)
+            nc.vector.tensor_copy(out=bo[:], in_=bo_spread[:])
 
         resid = {}
         o_grouped = {}
@@ -160,7 +155,7 @@ def tile_block_pa_kernel(
             adder = nc.vector if b in RESID_ON_VECTOR else nc.gpsimd
             resid[b, r] = work.tile([P, D], F32, name="resid_b")
             adder.tensor_tensor(
-                out=resid[b, r][:], in0=x_sb[b][:, r, :], in1=bias_all[:, 0:D], op=ALU.add
+                out=resid[b, r][:], in0=x_sb[b][:, r, :], in1=bo[:], op=ALU.add
             )
 
         o_turned = {}
@@ -308,13 +303,12 @@ def tile_block_pa_kernel(
 
         def finish_qkv(b, r, thirds=range(N_QKV)):
             for w in thirds:
-                cols = slice(D + w * D, D + (w + 1) * D)
                 if r == 0:
                     head_rows[b, w] = heads.tile([P, NH, R, HD], F32, name="head_rows_b")
                 nc.vector.tensor_tensor(
                     out=head_rows[b, w][:, :, r, :],
                     in0=qkv_accs[b, r, w][:].rearrange("p (n d) -> p n d", n=NH),
-                    in1=bias_all[:, cols].rearrange("p (n d) -> p n d", n=NH),
+                    in1=bqkv[:, w * D : (w + 1) * D].rearrange("p (n d) -> p n d", n=NH),
                     op=ALU.add,
                 )
                 if r == R - 1:
@@ -323,8 +317,7 @@ def tile_block_pa_kernel(
                         in_=head_rows[b, w][:].rearrange("p n r d -> p n (r d)"),
                     )
 
-        spread_bias(0, bo_rows[:])
-        copy_bias(0, nc.vector.tensor_copy)
+        spread_bo()
         turn_o(0)
         add_resid(1, 0)
         add_resid(1, 1)
@@ -337,20 +330,14 @@ def tile_block_pa_kernel(
         quantise_o(0)
         project_o(0)
         group_o(1)
-        spread_bias(1, bqkv_rows[:, 0 * D : 1 * D])
-        spread_bias(2, bqkv_rows[:, 1 * D : 2 * D])
-        spread_bias(3, bqkv_rows[:, 2 * D : 3 * D])
         finish_x_loc(0)
         quantise_o(1)
-        copy_bias(1, nc.vector.tensor_copy)
         project_o(1)
         turn_o(2)
         normalise(0, [0])
         normalise(0, [1])
         group_o(2)
         finish_x_loc(1)
-        copy_bias(2, nc.vector.tensor_copy)
-        copy_bias(3, nc.vector.tensor_copy)
         quantise_o(2)
         turn_h(0, 0)
         scale_h(0, 0)

@@ -22,7 +22,6 @@ N_ALL = D + N_QKV * D
 BLOCK_ROWS = 16
 EPS = 1e-5
 RESID_ON_VECTOR = (0,)
-REGROUP_ON_VECTOR = (0,)
 FLOPS = 2 * B * S * D * N_ALL
 
 
@@ -64,9 +63,9 @@ def tile_block_pa_kernel(
                 nc.sync.dma_start(out=o_b[:, r, :].rearrange("p (n d) -> p n d", n=NH), in_=by_r[r])
             o_sb[b] = o_b
 
-        def load_x(b):
+        def load_x(b, queue):
             x_b = batch.tile([P, R, D], BF16)
-            nc.sync.dma_start(
+            queue.dma_start(
                 out=x_b[:].rearrange("p r k -> p (r k)"),
                 in_=x[b].rearrange("(p r) k -> p (r k)", r=R),
             )
@@ -92,31 +91,31 @@ def tile_block_pa_kernel(
         wo_words = const.tile([P, D], U32, align_bytes=64)
         wqkv_words = const.tile([P, N_QKV * D], U32, align_bytes=64)
 
-        load_scales(wo_scales, Wo_l_scales[0])
-        nc.sync.dma_start(out=bo_rows[0:1, :], in_=bo_l.rearrange("(o n) -> o n", o=1))
         load_o(0)
         nc.sync.dma_start(
             out=wo_words[:].bitcast(I32),
             in_=Wo_l_words[0].rearrange("p n t -> p (n t)").bitcast(I32),
         )
-        load_x(0)
+        load_scales(wo_scales, Wo_l_scales[0])
+        nc.sync.dma_start(out=bo_rows[0:1, :], in_=bo_l.rearrange("(o n) -> o n", o=1))
         load_o(1)
-        load_x(1)
+        load_x(1, nc.sync)
         load_o(2)
-        load_x(2)
+        load_x(2, nc.sync)
         load_scales(wqkv_scales, Wqkv_g_scales[0])
         nc.sync.dma_start(
             out=wqkv_words[:].bitcast(I32),
             in_=Wqkv_g_words[0].rearrange("p n t -> p (n t)").bitcast(I32),
         )
         load_o(3)
-        load_x(3)
+        load_x(3, nc.sync)
         nc.sync.dma_start(out=bqkv[:], in_=bqkv_g.partition_broadcast(P))
 
         identity = const.tile([P, P], F32)
         masks.make_identity(nc, identity[:])
         gain_bf = const.tile([P, PACK], BF16)
         shift_bf = const.tile([P, PACK], BF16)
+        load_x(0, nc.gpsimd)
         nc.gpsimd.dma_start(out=gain_bf[:], in_=ln2_w.rearrange("(p t) -> p t", t=PACK))
         nc.gpsimd.dma_start(out=shift_bf[:], in_=ln2_b.rearrange("(p t) -> p t", t=PACK))
         gain = const.tile([P, PACK], F32)
@@ -273,8 +272,7 @@ def tile_block_pa_kernel(
 
         def group_h(b, r):
             h_grouped[b, r] = work.tile([P, P, PACK], BF16, align_bytes=64, name="h_grouped_b")
-            copy = nc.vector.tensor_copy if b in REGROUP_ON_VECTOR else nc.scalar.copy
-            copy(out=h_grouped[b, r][:], in_=h_t[b, r][:].rearrange("p t c -> p c t"))
+            nc.scalar.copy(out=h_grouped[b, r][:], in_=h_t[b, r][:].rearrange("p t c -> p c t"))
 
         def quantise_h(b, r):
             h_codes[b, r] = work.tile([P, P], U32, align_bytes=64, name="h_codes_b")
@@ -311,29 +309,33 @@ def tile_block_pa_kernel(
                     in1=bqkv[:, w * D : (w + 1) * D].rearrange("p (n d) -> p n d", n=NH),
                     op=ALU.add,
                 )
-                if r == R - 1:
+                if b == B - 1:
+                    nc.sync.dma_start(
+                        out=qkv_out[w][b].rearrange("n (p r) d -> r p n d", r=R)[r],
+                        in_=head_rows[b, w][:, :, r, :],
+                    )
+                elif r == R - 1:
                     nc.sync.dma_start(
                         out=qkv_out[w][b].rearrange("n (p r) d -> p n (r d)", r=R),
                         in_=head_rows[b, w][:].rearrange("p n r d -> p n (r d)"),
                     )
 
-        spread_bo()
         turn_o(0)
+        spread_bo()
         add_resid(1, 0)
         add_resid(1, 1)
-        add_resid(2, 0)
         widen_affine()
-        turn_o(1)
         group_o(0)
-        add_resid(0, 0)
-        add_resid(0, 1)
         quantise_o(0)
         project_o(0)
-        group_o(1)
+        turn_o(1)
+        add_resid(0, 0)
+        add_resid(0, 1)
         finish_x_loc(0)
+        group_o(1)
         quantise_o(1)
-        project_o(1)
         turn_o(2)
+        project_o(1)
         normalise(0, [0])
         normalise(0, [1])
         group_o(2)
@@ -341,16 +343,17 @@ def tile_block_pa_kernel(
         quantise_o(2)
         turn_h(0, 0)
         scale_h(0, 0)
+        group_h(0, 0)
         turn_h(0, 1)
         project_o(2)
         scale_h(0, 1)
-        group_h(0, 0)
+        group_h(0, 1)
+        add_resid(2, 0)
+        add_resid(2, 1)
         quantise_h(0, 0)
         project_qkv(0, 0)
         turn_o(3)
-        add_resid(2, 1)
         finish_x_loc(2)
-        group_h(0, 1)
         quantise_h(0, 1)
         project_qkv(0, 1)
         normalise(1)

@@ -50,7 +50,7 @@ def tile_block_pa_kernel(
         const = ctx.enter_context(tc.tile_pool(name="const", bufs=1))
         batch = ctx.enter_context(tc.tile_pool(name="batch", bufs=B))
         work = ctx.enter_context(tc.tile_pool(name="work", bufs=B * R))
-        heads = ctx.enter_context(tc.tile_pool(name="heads", bufs=B * N_QKV))
+        heads = ctx.enter_context(tc.tile_pool(name="heads", bufs=B * R * N_QKV))
         psum = ctx.enter_context(tc.psum_pool(name="psum", bufs=8))
 
         o_sb = {}
@@ -71,10 +71,10 @@ def tile_block_pa_kernel(
             )
             x_sb[b] = x_b
 
-        wo_scales = const.tile([P, D], U8, align_bytes=64)
-        nc.vector.memset(wo_scales[:].bitcast(I32), 0)
         bo_rows = const.tile([P, D], BF16)
         nc.vector.memset(bo_rows[:], 0.0)
+        wo_scales = const.tile([P, D], U8, align_bytes=64)
+        nc.vector.memset(wo_scales[:].bitcast(I32), 0)
         ones = const.tile([P, P], BF16)
         nc.vector.memset(ones[:], 1.0)
         wqkv_scales = const.tile([P, N_QKV * D], U8, align_bytes=64)
@@ -96,8 +96,8 @@ def tile_block_pa_kernel(
             out=wo_words[:].bitcast(I32),
             in_=Wo_l_words[0].rearrange("p n t -> p (n t)").bitcast(I32),
         )
-        load_scales(wo_scales, Wo_l_scales[0])
         nc.sync.dma_start(out=bo_rows[0:1, :], in_=bo_l.rearrange("(o n) -> o n", o=1))
+        load_scales(wo_scales, Wo_l_scales[0])
         load_o(1)
         load_x(1, nc.sync)
         load_o(2)
@@ -131,10 +131,12 @@ def tile_block_pa_kernel(
         )
 
         bo = const.tile([P, D], F32)
+        bo_spread = psum.tile([P, D], F32, tag="bank")
 
         def spread_bo():
-            bo_spread = psum.tile([P, D], F32, tag="bank")
             nc.tensor.matmul(out=bo_spread[:], lhsT=ones[:], rhs=bo_rows[:], start=True, stop=True)
+
+        def copy_bo():
             nc.vector.tensor_copy(out=bo[:], in_=bo_spread[:])
 
         resid = {}
@@ -284,7 +286,6 @@ def tile_block_pa_kernel(
             )
 
         qkv_accs = {}
-        head_rows = {}
 
         def project_qkv(b, r, thirds=range(N_QKV)):
             for w in thirds:
@@ -301,33 +302,27 @@ def tile_block_pa_kernel(
 
         def finish_qkv(b, r, thirds=range(N_QKV)):
             for w in thirds:
-                if r == 0:
-                    head_rows[b, w] = heads.tile([P, NH, R, HD], F32, name="head_rows_b")
+                head_rows = heads.tile([P, NH, HD], F32)
                 nc.vector.tensor_tensor(
-                    out=head_rows[b, w][:, :, r, :],
+                    out=head_rows[:],
                     in0=qkv_accs[b, r, w][:].rearrange("p (n d) -> p n d", n=NH),
                     in1=bqkv[:, w * D : (w + 1) * D].rearrange("p (n d) -> p n d", n=NH),
                     op=ALU.add,
                 )
-                if b == B - 1:
-                    nc.sync.dma_start(
-                        out=qkv_out[w][b].rearrange("n (p r) d -> r p n d", r=R)[r],
-                        in_=head_rows[b, w][:, :, r, :],
-                    )
-                elif r == R - 1:
-                    nc.sync.dma_start(
-                        out=qkv_out[w][b].rearrange("n (p r) d -> p n (r d)", r=R),
-                        in_=head_rows[b, w][:].rearrange("p n r d -> p n (r d)"),
-                    )
+                nc.sync.dma_start(
+                    out=qkv_out[w][b].rearrange("n (p r) d -> r p n d", r=R)[r],
+                    in_=head_rows[:],
+                )
 
         turn_o(0)
         spread_bo()
-        add_resid(1, 0)
-        add_resid(1, 1)
-        widen_affine()
         group_o(0)
         quantise_o(0)
         project_o(0)
+        copy_bo()
+        add_resid(1, 0)
+        add_resid(1, 1)
+        widen_affine()
         turn_o(1)
         add_resid(0, 0)
         add_resid(0, 1)

@@ -202,10 +202,11 @@ def tile_block_pa_kernel(
 
         token_sums = {}
 
-        def finish_x_loc(b):
-            x_loc[b] = batch.tile([P, R, D], F32, name="x_loc_b")
-            token_sums[b] = batch.tile([P, R], F32, name="token_sums_b")
-            for r in range(R):
+        def finish_x_loc(b, tokens=range(R)):
+            if tokens[0] == 0:
+                x_loc[b] = batch.tile([P, R, D], F32, name="x_loc_b")
+                token_sums[b] = batch.tile([P, R], F32, name="token_sums_b")
+            for r in tokens:
                 nc.vector.scalar_tensor_tensor(
                     out=x_loc[b][:, r, :],
                     in0=x_accs[b][r][:],
@@ -215,10 +216,11 @@ def tile_block_pa_kernel(
                     op1=ALU.add,
                     accum_out=token_sums[b][:, r : r + 1],
                 )
-            nc.sync.dma_start(
-                out=out_0[b].rearrange("(p r) k -> p (r k)", r=R),
-                in_=x_loc[b][:].rearrange("p r k -> p (r k)"),
-            )
+            if tokens[-1] == R - 1:
+                nc.sync.dma_start(
+                    out=out_0[b].rearrange("(p r) k -> p (r k)", r=R),
+                    in_=x_loc[b][:].rearrange("p r k -> p (r k)"),
+                )
 
         def normalise(b, tokens=range(R)):
             n = len(tokens)
@@ -366,9 +368,10 @@ def tile_block_pa_kernel(
         group_h(1, 0)
         scale_h(1, 1)
         group_h(1, 1)
-        finish_x_loc(3)
+        finish_x_loc(3, [0])
         quantise_h(1, 0)
         project_qkv(1, 0)
+        finish_x_loc(3, [1])
         quantise_h(1, 1)
         turn_h(2, 0)
         turn_h(2, 1)

@@ -50,7 +50,7 @@ def tile_block_pa_kernel(
         const = ctx.enter_context(tc.tile_pool(name="const", bufs=1))
         batch = ctx.enter_context(tc.tile_pool(name="batch", bufs=B))
         work = ctx.enter_context(tc.tile_pool(name="work", bufs=B * R))
-        heads = ctx.enter_context(tc.tile_pool(name="heads", bufs=B * R * N_QKV))
+        heads = ctx.enter_context(tc.tile_pool(name="heads", bufs=B * N_QKV))
         psum = ctx.enter_context(tc.psum_pool(name="psum", bufs=8))
 
         o_sb = {}
@@ -302,19 +302,23 @@ def tile_block_pa_kernel(
                     stop=True,
                 )
 
+        head_rows = {}
+
         def finish_qkv(b, r, thirds=range(N_QKV)):
             for w in thirds:
-                head_rows = heads.tile([P, NH, HD], F32)
+                if r == 0:
+                    head_rows[b, w] = heads.tile([P, NH, R, HD], F32, name="head_rows_b")
                 nc.vector.tensor_tensor(
-                    out=head_rows[:],
+                    out=head_rows[b, w][:, :, r, :],
                     in0=qkv_accs[b, r, w][:].rearrange("p (n d) -> p n d", n=NH),
                     in1=bqkv[:, w * D : (w + 1) * D].rearrange("p (n d) -> p n d", n=NH),
                     op=ALU.add,
                 )
-                nc.sync.dma_start(
-                    out=qkv_out[w][b].rearrange("n (p r) d -> r p n d", r=R)[r],
-                    in_=head_rows[:],
-                )
+                if r == R - 1:
+                    nc.sync.dma_start(
+                        out=qkv_out[w][b].rearrange("n (p r) d -> p n (r d)", r=R),
+                        in_=head_rows[b, w][:].rearrange("p n r d -> p n (r d)"),
+                    )
 
         turn_o(0)
         spread_bo()
@@ -350,6 +354,8 @@ def tile_block_pa_kernel(
         quantise_h(0, 0)
         project_qkv(0, 0)
         turn_o(3)
+        add_resid(3, 0)
+        add_resid(3, 1)
         finish_x_loc(2)
         quantise_h(0, 1)
         project_qkv(0, 1)
@@ -357,24 +363,21 @@ def tile_block_pa_kernel(
         group_o(3)
         finish_qkv(0, 0)
         quantise_o(3)
-        add_resid(3, 0)
-        add_resid(3, 1)
         normalise(2)
         turn_h(1, 0)
         turn_h(1, 1)
         project_o(3)
         finish_qkv(0, 1)
+        finish_x_loc(3)
+        turn_h(2, 0)
+        turn_h(2, 1)
         scale_h(1, 0)
         group_h(1, 0)
         scale_h(1, 1)
         group_h(1, 1)
-        finish_x_loc(3, [0])
         quantise_h(1, 0)
         project_qkv(1, 0)
-        finish_x_loc(3, [1])
         quantise_h(1, 1)
-        turn_h(2, 0)
-        turn_h(2, 1)
         project_qkv(1, 1)
         normalise(3)
         scale_h(2, 0)
@@ -385,12 +388,12 @@ def tile_block_pa_kernel(
         finish_qkv(1, 1, [0])
         finish_qkv(1, 1, [1])
         quantise_h(2, 0)
+        turn_h(3, 0)
+        turn_h(3, 1)
         project_qkv(2, 0)
         finish_qkv(1, 1, [2])
         finish_qkv(2, 0, [0])
         finish_qkv(2, 0, [1])
-        turn_h(3, 0)
-        turn_h(3, 1)
         quantise_h(2, 1)
         project_qkv(2, 1)
         scale_h(3, 0)

@@ -21,7 +21,7 @@ N_QKV = 3
 N_ALL = D + N_QKV * D
 BLOCK_ROWS = 16
 EPS = 1e-5
-RESID_ON_VECTOR = (0,)
+RESID_ON_VECTOR = (0, 1, 2)
 FLOPS = 2 * B * S * D * N_ALL
 
 
@@ -92,12 +92,12 @@ def tile_block_pa_kernel(
         wqkv_words = const.tile([P, N_QKV * D], U32, align_bytes=64)
 
         load_o(0)
+        nc.sync.dma_start(out=bo_rows[0:1, :], in_=bo_l.rearrange("(o n) -> o n", o=1))
+        load_scales(wo_scales, Wo_l_scales[0])
         nc.sync.dma_start(
             out=wo_words[:].bitcast(I32),
             in_=Wo_l_words[0].rearrange("p n t -> p (n t)").bitcast(I32),
         )
-        nc.sync.dma_start(out=bo_rows[0:1, :], in_=bo_l.rearrange("(o n) -> o n", o=1))
-        load_scales(wo_scales, Wo_l_scales[0])
         load_o(1)
         load_x(1, nc.sync)
         load_o(2)
@@ -122,8 +122,8 @@ def tile_block_pa_kernel(
         shift = const.tile([P, PACK], F32)
 
         def widen_affine():
-            nc.gpsimd.tensor_copy(out=gain[:], in_=gain_bf[:])
-            nc.gpsimd.tensor_copy(out=shift[:], in_=shift_bf[:])
+            nc.scalar.copy(out=gain[:], in_=gain_bf[:])
+            nc.scalar.copy(out=shift[:], in_=shift_bf[:])
 
         table = const.tile([P, 1], F32)
         nc.scalar.activation(
@@ -326,22 +326,24 @@ def tile_block_pa_kernel(
         quantise_o(0)
         project_o(0)
         copy_bo()
-        add_resid(1, 0)
-        add_resid(1, 1)
-        widen_affine()
         turn_o(1)
         add_resid(0, 0)
         add_resid(0, 1)
         finish_x_loc(0)
         group_o(1)
         quantise_o(1)
+        add_resid(1, 0)
+        add_resid(1, 1)
         turn_o(2)
         project_o(1)
         normalise(0, [0])
         normalise(0, [1])
         group_o(2)
+        widen_affine()
         finish_x_loc(1)
         quantise_o(2)
+        add_resid(2, 0)
+        add_resid(2, 1)
         turn_h(0, 0)
         scale_h(0, 0)
         group_h(0, 0)
@@ -349,8 +351,6 @@ def tile_block_pa_kernel(
         project_o(2)
         scale_h(0, 1)
         group_h(0, 1)
-        add_resid(2, 0)
-        add_resid(2, 1)
         quantise_h(0, 0)
         project_qkv(0, 0)
         turn_o(3)
@@ -386,8 +386,8 @@ def tile_block_pa_kernel(
         group_h(2, 1)
         finish_qkv(1, 0)
         finish_qkv(1, 1, [0])
-        finish_qkv(1, 1, [1])
         quantise_h(2, 0)
+        finish_qkv(1, 1, [1])
         turn_h(3, 0)
         turn_h(3, 1)
         project_qkv(2, 0)
@@ -402,8 +402,8 @@ def tile_block_pa_kernel(
         group_h(3, 1)
         finish_qkv(2, 0, [2])
         finish_qkv(2, 1, [0])
-        finish_qkv(2, 1, [1])
         quantise_h(3, 0)
+        finish_qkv(2, 1, [1])
         project_qkv(3, 0)
         finish_qkv(2, 1, [2])
         finish_qkv(3, 0, [0])

from contextlib import ExitStack

import concourse.masks as masks
import concourse.mybir as mybir

F32 = mybir.dt.float32
BF16 = mybir.dt.bfloat16
I32 = mybir.dt.int32
U32 = mybir.dt.uint32
U8 = mybir.dt.uint8
FP8X4 = mybir.dt.float8_e4m3fn_x4
ALU = mybir.AluOpType
ACT = mybir.ActivationFunctionType

B, S, D, NH, HD = 4, 256, 512, 4, 128
P = 128
R = S // P
PACK = 4
PAIR = 2
N_QKV = 3
N_ALL = D + N_QKV * D
BLOCK_ROWS = 16
EPS = 1e-5
RESID_ON_VECTOR = (0, 1, 2)
FLOPS = 2 * B * S * D * N_ALL


def tile_block_pa_kernel(
    tc,
    o_loc,
    x,
    Wo_l_words,
    Wo_l_scales,
    bo_l,
    ln2_w,
    ln2_b,
    Wqkv_g_words,
    Wqkv_g_scales,
    bqkv_g,
    out_0,
    out_1,
    out_2,
    out_3,
):
    nc = tc.nc
    qkv_out = [out_1, out_2, out_3]

    with ExitStack() as ctx:
        ctx.enter_context(tc.manual_schedule())
        const = ctx.enter_context(tc.tile_pool(name="const", bufs=1))
        batch = ctx.enter_context(tc.tile_pool(name="batch", bufs=B))
        work = ctx.enter_context(tc.tile_pool(name="work", bufs=B * R))
        heads = ctx.enter_context(tc.tile_pool(name="heads", bufs=B * N_QKV))
        psum = ctx.enter_context(tc.psum_pool(name="psum", bufs=8))

        o_sb = {}
        x_sb = {}

        def load_o(b):
            o_b = batch.tile([P, R, D], BF16)
            by_r = o_loc[b].rearrange("n (p r) d -> r p n d", r=R)
            for r in range(R):
                nc.sync.dma_start(out=o_b[:, r, :].rearrange("p (n d) -> p n d", n=NH), in_=by_r[r])
            o_sb[b] = o_b

        def load_x(b, queue):
            x_b = batch.tile([P, R, D], BF16)
            queue.dma_start(
                out=x_b[:].rearrange("p r k -> p (r k)"),
                in_=x[b].rearrange("(p r) k -> p (r k)", r=R),
            )
            x_sb[b] = x_b

        bo_rows = const.tile([P, D], BF16)
        nc.vector.memset(bo_rows[:], 0.0)
        wo_scales = const.tile([P, D], U8, align_bytes=64)
        nc.vector.memset(wo_scales[:].bitcast(I32), 0)
        ones = const.tile([P, P], BF16)
        nc.vector.memset(ones[:], 1.0)
        wqkv_scales = const.tile([P, N_QKV * D], U8, align_bytes=64)
        nc.vector.memset(wqkv_scales[:].bitcast(I32), 0)
        bqkv = const.tile([P, N_QKV * D], BF16)

        def load_scales(scales, rows):
            for j in range(4):
                nc.sync.dma_start(
                    out=scales[j:P:32, :].bitcast(I32),
                    in_=rows[j:BLOCK_ROWS:4, :].bitcast(I32),
                )

        wo_words = const.tile([P, D], U32, align_bytes=64)
        wqkv_words = const.tile([P, N_QKV * D], U32, align_bytes=64)

        load_o(0)
        nc.sync.dma_start(out=bo_rows[0:1, :], in_=bo_l.rearrange("(o n) -> o n", o=1))
        load_scales(wo_scales, Wo_l_scales[0])
        nc.sync.dma_start(
            out=wo_words[:].bitcast(I32),
            in_=Wo_l_words[0].rearrange("p n t -> p (n t)").bitcast(I32),
        )
        load_o(1)
        load_x(1, nc.sync)
        load_o(2)
        load_x(2, nc.sync)
        load_scales(wqkv_scales, Wqkv_g_scales[0])
        nc.sync.dma_start(
            out=wqkv_words[:].bitcast(I32),
            in_=Wqkv_g_words[0].rearrange("p n t -> p (n t)").bitcast(I32),
        )
        load_o(3)
        load_x(3, nc.sync)
        nc.sync.dma_start(out=bqkv[:], in_=bqkv_g.partition_broadcast(P))

        identity = const.tile([P, P], F32)
        masks.make_identity(nc, identity[:])
        gain_bf = const.tile([P, PACK], BF16)
        shift_bf = const.tile([P, PACK], BF16)
        load_x(0, nc.gpsimd)
        nc.gpsimd.dma_start(out=gain_bf[:], in_=ln2_w.rearrange("(p t) -> p t", t=PACK))
        nc.gpsimd.dma_start(out=shift_bf[:], in_=ln2_b.rearrange("(p t) -> p t", t=PACK))
        gain = const.tile([P, PACK], F32)
        shift = const.tile([P, PACK], F32)

        def widen_affine():
            nc.scalar.copy(out=gain[:], in_=gain_bf[:])
            nc.scalar.copy(out=shift[:], in_=shift_bf[:])

        table = const.tile([P, 1], F32)
        nc.scalar.activation(
            out=table[:], in_=ones[:, 0:1], func=ACT.Abs_reciprocal_sqrt, bias=EPS, scale=1.0 / D
        )

        bo = const.tile([P, D], F32)
        bo_spread = psum.tile([P, D], F32, tag="bank")

        def spread_bo():
            nc.tensor.matmul(out=bo_spread[:], lhsT=ones[:], rhs=bo_rows[:], start=True, stop=True)

        def copy_bo():
            nc.vector.tensor_copy(out=bo[:], in_=bo_spread[:])

        resid = {}
        o_grouped = {}
        o_codes = {}
        o_scales = {}
        x_loc = {}
        x_accs = {}
        minus_mean = {}
        normed = {}
        h_t = {}
        h_grouped = {}
        h_codes = {}
        h_scales = {}

        def add_resid(b, r):
            adder = nc.vector if b in RESID_ON_VECTOR else nc.gpsimd
            resid[b, r] = work.tile([P, D], F32, name="resid_b")
            adder.tensor_tensor(
                out=resid[b, r][:], in0=x_sb[b][:, r, :], in1=bo[:], op=ALU.add
            )

        o_turned = {}

        def turn_o(b):
            o_turned[b] = psum.tile([P, R, PAIR, P], F32, tag="bank", name="o_turned_b")
            for r in range(R):
                words = o_sb[b][:, r, :].bitcast(F32)
                for u in range(PAIR):
                    nc.tensor.transpose(
                        out=o_turned[b][:, r, u, :], in_=words[:, u : D // PAIR : PAIR], identity=identity[:]
                    )

        def group_o(b):
            o_grouped[b] = work.tile([P, R * P * PACK], BF16, align_bytes=64, name="o_grouped_b")
            nc.scalar.copy(
                out=o_grouped[b][:].bitcast(F32).rearrange("p (r c u) -> p r c u", r=R, u=PAIR),
                in_=o_turned[b][:].rearrange("p r u c -> p r c u"),
            )

        def quantise_o(b):
            o_codes[b] = work.tile([P, R * P], U32, align_bytes=64, name="o_codes_b")
            o_scales[b] = work.tile([P, R * P], U8, align_bytes=64, name="o_scales_b")
            nc.vector.quantize_mx(
                out=o_codes[b][:].bitcast(FP8X4), scales=o_scales[b][:], in_=o_grouped[b][:]
            )

        def project_o(b):
            x_accs[b] = []
            for r in range(R):
                tokens = slice(r * P, (r + 1) * P)
                x_acc = psum.tile([P, D], F32, tag="bank")
                nc.tensor.matmul_mx(
                    out=x_acc[:],
                    lhsT=o_codes[b][:, tokens].bitcast(FP8X4),
                    lhsT_scale=o_scales[b][:, tokens],
                    rhs=wo_words[:].bitcast(FP8X4),
                    rhs_scale=wo_scales[:],
                    start=True,
                    stop=True,
                )
                x_accs[b].append(x_acc)

        token_sums = {}

        def finish_x_loc(b, tokens=range(R)):
            if tokens[0] == 0:
                x_loc[b] = batch.tile([P, R, D], F32, name="x_loc_b")
                token_sums[b] = batch.tile([P, R], F32, name="token_sums_b")
            for r in tokens:
                nc.vector.scalar_tensor_tensor(
                    out=x_loc[b][:, r, :],
                    in0=x_accs[b][r][:],
                    scalar=1.0,
                    in1=resid[b, r][:],
                    op0=ALU.mult,
                    op1=ALU.add,
                    accum_out=token_sums[b][:, r : r + 1],
                )
            if tokens[-1] == R - 1:
                nc.sync.dma_start(
                    out=out_0[b].rearrange("(p r) k -> p (r k)", r=R),
                    in_=x_loc[b][:].rearrange("p r k -> p (r k)"),
                )

        def normalise(b, tokens=range(R)):
            n = len(tokens)
            minus_mean = work.tile([P, n], F32)
            sum_sq = work.tile([P, n], F32)
            rstd = work.tile([P, n], F32)
            nc.scalar.mul(
                out=minus_mean[:], in_=token_sums[b][:, tokens[0] : tokens[0] + n], mul=-1.0 / D
            )
            for i in range(n):
                squares = work.tile([P, D], BF16)
                nc.scalar.activation(
                    out=squares[:],
                    in_=x_loc[b][:, tokens[i], :],
                    func=ACT.Square,
                    bias=minus_mean[:, i : i + 1],
                    scale=1.0,
                    accum_out=sum_sq[:, i : i + 1],
                )
            nc.scalar.activation(
                out=rstd[:], in_=sum_sq[:], func=ACT.Abs_reciprocal_sqrt, bias=EPS, scale=1.0 / D
            )
            for i in range(n):
                normed[b, tokens[i]] = work.tile([P, PACK, P], F32, name="normed_b")
                nc.gpsimd.tensor_scalar(
                    out=normed[b, tokens[i]][:],
                    in0=x_loc[b][:, tokens[i], :].rearrange("p (q t) -> p t q", t=PACK),
                    scalar1=minus_mean[:, i : i + 1],
                    scalar2=rstd[:, i : i + 1],
                    op0=ALU.add,
                    op1=ALU.mult,
                )

        normed_turned = {}

        def turn_h(b, r):
            normed_turned[b, r] = psum.tile([P, PACK, P], F32, tag="bank", name="normed_turned_b")
            for t in range(PACK):
                nc.tensor.transpose(
                    out=normed_turned[b, r][:, t, :], in_=normed[b, r][:, t, :], identity=identity[:]
                )

        def scale_h(b, r):
            h_t[b, r] = work.tile([P, PACK, P], BF16, name="h_t_b")
            for t in range(PACK):
                nc.scalar.activation(
                    out=h_t[b, r][:, t, :],
                    in_=normed_turned[b, r][:, t, :],
                    func=ACT.Identity,
                    scale=gain[:, t : t + 1],
                    bias=shift[:, t : t + 1],
                )

        def group_h(b, r):
            h_grouped[b, r] = work.tile([P, P, PACK], BF16, align_bytes=64, name="h_grouped_b")
            nc.scalar.copy(out=h_grouped[b, r][:], in_=h_t[b, r][:].rearrange("p t c -> p c t"))

        def quantise_h(b, r):
            h_codes[b, r] = work.tile([P, P], U32, align_bytes=64, name="h_codes_b")
            h_scales[b, r] = work.tile([P, P], U8, align_bytes=64, name="h_scales_b")
            nc.vector.quantize_mx(
                out=h_codes[b, r][:].bitcast(FP8X4),
                scales=h_scales[b, r][:],
                in_=h_grouped[b, r][:].rearrange("p c t -> p (c t)"),
            )

        qkv_accs = {}

        def project_qkv(b, r, thirds=range(N_QKV)):
            for w in thirds:
                qkv_accs[b, r, w] = psum.tile([P, D], F32, tag="bank", name="qkv_acc")
                nc.tensor.matmul_mx(
                    out=qkv_accs[b, r, w][:],
                    lhsT=h_codes[b, r][:].bitcast(FP8X4),
                    lhsT_scale=h_scales[b, r][:],
                    rhs=wqkv_words[:, w * D : (w + 1) * D].bitcast(FP8X4),
                    rhs_scale=wqkv_scales[:, w * D : (w + 1) * D],
                    start=True,
                    stop=True,
                )

        head_rows = {}

        def finish_qkv(b, r, thirds=range(N_QKV)):
            for w in thirds:
                if r == 0:
                    head_rows[b, w] = heads.tile([P, NH, R, HD], F32, name="head_rows_b")
                nc.vector.tensor_tensor(
                    out=head_rows[b, w][:, :, r, :],
                    in0=qkv_accs[b, r, w][:].rearrange("p (n d) -> p n d", n=NH),
                    in1=bqkv[:, w * D : (w + 1) * D].rearrange("p (n d) -> p n d", n=NH),
                    op=ALU.add,
                )
                if r == R - 1:
                    nc.sync.dma_start(
                        out=qkv_out[w][b].rearrange("n (p r) d -> p n (r d)", r=R),
                        in_=head_rows[b, w][:].rearrange("p n r d -> p n (r d)"),
                    )

        turn_o(0)
        spread_bo()
        group_o(0)
        quantise_o(0)
        project_o(0)
        copy_bo()
        turn_o(1)
        add_resid(0, 0)
        add_resid(0, 1)
        finish_x_loc(0)
        group_o(1)
        quantise_o(1)
        add_resid(1, 0)
        add_resid(1, 1)
        turn_o(2)
        project_o(1)
        normalise(0, [0])
        normalise(0, [1])
        group_o(2)
        widen_affine()
        finish_x_loc(1)
        quantise_o(2)
        add_resid(2, 0)
        add_resid(2, 1)
        turn_h(0, 0)
        scale_h(0, 0)
        group_h(0, 0)
        turn_h(0, 1)
        project_o(2)
        scale_h(0, 1)
        group_h(0, 1)
        quantise_h(0, 0)
        project_qkv(0, 0)
        turn_o(3)
        add_resid(3, 0)
        add_resid(3, 1)
        finish_x_loc(2)
        quantise_h(0, 1)
        project_qkv(0, 1)
        normalise(1)
        group_o(3)
        finish_qkv(0, 0)
        quantise_o(3)
        normalise(2)
        turn_h(1, 0)
        turn_h(1, 1)
        project_o(3)
        finish_qkv(0, 1)
        finish_x_loc(3)
        turn_h(2, 0)
        turn_h(2, 1)
        scale_h(1, 0)
        group_h(1, 0)
        scale_h(1, 1)
        group_h(1, 1)
        quantise_h(1, 0)
        project_qkv(1, 0)
        quantise_h(1, 1)
        project_qkv(1, 1)
        normalise(3)
        scale_h(2, 0)
        group_h(2, 0)
        scale_h(2, 1)
        group_h(2, 1)
        finish_qkv(1, 0)
        finish_qkv(1, 1, [0])
        quantise_h(2, 0)
        finish_qkv(1, 1, [1])
        turn_h(3, 0)
        turn_h(3, 1)
        project_qkv(2, 0)
        finish_qkv(1, 1, [2])
        finish_qkv(2, 0, [0])
        finish_qkv(2, 0, [1])
        quantise_h(2, 1)
        project_qkv(2, 1)
        scale_h(3, 0)
        group_h(3, 0)
        scale_h(3, 1)
        group_h(3, 1)
        finish_qkv(2, 0, [2])
        finish_qkv(2, 1, [0])
        quantise_h(3, 0)
        finish_qkv(2, 1, [1])
        project_qkv(3, 0)
        finish_qkv(2, 1, [2])
        finish_qkv(3, 0, [0])
        finish_qkv(3, 0, [1])
        quantise_h(3, 1)
        project_qkv(3, 1)
        finish_qkv(3, 0, [2])
        finish_qkv(3, 1)
